import numpy as np
import ml_dtypes


def mxq(x, axis, fmt="e4m3"):
    dtype, down = {"e4m3": (ml_dtypes.float8_e4m3fn, 7), "e5m2": (ml_dtypes.float8_e5m2, 14)}[fmt]
    v = np.moveaxis(np.asarray(x, np.float32).astype(ml_dtypes.bfloat16).astype(np.float64), axis, -1)
    blocks = v.reshape(v.shape[:-1] + (-1, 32))
    amax = np.abs(blocks).max(-1, keepdims=True)
    byte = np.maximum(np.where(amax > 0, np.frexp(amax)[1] - 1 + 127, 0) - down, 1)
    scale = np.exp2(byte - 127.0)
    codes = (blocks / scale).astype(np.float32).astype(dtype).astype(np.float64)
    return np.moveaxis((codes * scale).reshape(v.shape), -1, axis)


WIDE = False


def mx_kscale(k):
    if not WIDE:
        return np.ones(k)
    levels = np.array([10, -10, 5, -5, 0])
    a = np.random.permutation(np.resize(levels, k // 512 * 4)).reshape(k // 512, 4)
    idx = np.arange(k)
    return np.exp2(a[idx // 512, idx % 128 // 32])


BF16 = ml_dtypes.bfloat16


def bf(x):
    return np.asarray(x, np.float32).astype(BF16)


def f64(x):
    return np.asarray(x).astype(np.float64)


B, S, D, H = 8, 512, 1024, 512


def setup_inputs():
    s, t = mx_kscale(D), mx_kscale(H)
    return {"audio_feature": bf(np.random.standard_normal((B, S, D)) * s),
            "W_phi": bf(np.random.standard_normal((D, H)) / np.sqrt(D) / s[:, None] * t),
            "b_phi": bf(np.random.standard_normal(H) * 0.2 * t),
            "W_theta": bf(np.random.standard_normal((D, H)) / np.sqrt(D) / s[:, None] / t),
            "b_theta": bf(np.random.standard_normal(H) * 0.2 / t)}


def reference(audio_feature, W_phi, b_phi, W_theta, b_theta):
    xq = mxq(f64(audio_feature), 2, "e4m3")
    phi_a = (xq @ mxq(f64(W_phi), 0, "e4m3")) + f64(b_phi)
    theta_a = (xq @ mxq(f64(W_theta), 0, "e4m3")) + f64(b_theta)
    scores = (mxq(phi_a, 2, "e4m3") @ mxq(theta_a, 2, "e4m3").transpose(0, 2, 1)) / np.sqrt(D)
    scores = np.maximum(scores, 0.0)
    return (scores + scores.transpose(0, 2, 1)) * 0.5

@@ -1,0 +1,216 @@
+import math
+from contextlib import ExitStack
+
+import concourse.mybir as mybir
+from concourse.masks import make_identity
+
+F32 = mybir.dt.float32
+BF16 = mybir.dt.bfloat16
+U32 = mybir.dt.uint32
+U8 = mybir.dt.uint8
+FP8X4 = mybir.dt.float8_e4m3fn_x4
+ACT = mybir.ActivationFunctionType
+ALU = mybir.AluOpType
+
+P = 128
+PACK = 4
+K_PASS = P * PACK
+
+B, S, D, H = 8, 512, 1024, 512
+D_PASSES = D // K_PASS
+ROW_TILES = S // P
+H_TILES = H // P
+assert H_TILES == PACK
+PHI, THETA = 0, 1
+HALF_OVER_SQRT_D = 0.5 / math.sqrt(D)
+
+FLOPS = 2 * B * S * D * (2 * H) + 2 * B * S * S * H
+
+
+SCORE_LAG = 3
+
+
+def tile_selfattention_pa_t_kernel(tc, audio_feature, W_phi, b_phi, W_theta, b_theta, out):
+    nc = tc.nc
+    with ExitStack() as ctx:
+        const = ctx.enter_context(tc.tile_pool(name="const", bufs=1))
+        w_stage = ctx.enter_context(tc.tile_pool(name="w_stage", bufs=2))
+        x_in = ctx.enter_context(tc.tile_pool(name="x_in", bufs=B))
+        x_mx = ctx.enter_context(tc.tile_pool(name="x_mx", bufs=2))
+        hid = ctx.enter_context(tc.tile_pool(name="hid", bufs=3))
+        hid_mx = ctx.enter_context(tc.tile_pool(name="hid_mx", bufs=6))
+        ends = ctx.enter_context(tc.tile_pool(name="ends", bufs=6))
+        psum = ctx.enter_context(tc.psum_pool(name="psum", bufs=8))
+        ctx.enter_context(tc.manual_schedule())
+
+        bias_rows_bf = const.tile([P, P], BF16)
+        nc.vector.memset(bias_rows_bf[:], 0.0)
+        nc.scalar.dma_start(out=bias_rows_bf[0:H_TILES, :], in_=b_phi.rearrange("(m p) -> m p", p=P))
+        nc.scalar.dma_start(
+            out=bias_rows_bf[H_TILES : 2 * H_TILES, :], in_=b_theta.rearrange("(m p) -> m p", p=P)
+        )
+
+        def load_weight(weight):
+            w_raw = w_stage.tile([P, D_PASSES * PACK, H], BF16, name="w_raw")
+            for g in range(D_PASSES):
+                nc.sync.dma_start(
+                    out=w_raw[:, PACK * g : PACK * (g + 1), :].rearrange("q (u e) h -> q u (e h)", e=2),
+                    in_=weight[K_PASS * g : K_PASS * (g + 1), :].rearrange("(u q e) h -> q u (e h)", q=P, e=2),
+                )
+            return w_raw
+
+        def load_x(b):
+            x_sb = x_in.tile([P, ROW_TILES, D], BF16, name="x_sb")
+            rows = audio_feature[b].rearrange("(r p) d -> p r d", p=P)
+            for half in range(2):
+                nc.sync.dma_start(out=x_sb[:, 2 * half : 2 * half + 2, :], in_=rows[:, 2 * half : 2 * half + 2, :])
+            return x_sb
+
+        w_raws = [load_weight(W_phi)]
+        x_tiles = [load_x(0)]
+        w_raws.append(load_weight(W_theta))
+        for b in range(1, B):
+            x_tiles.append(load_x(b))
+
+        ident = const.tile([P, P], F32)
+        make_identity(nc, ident[:])
+
+        bias_rows = const.tile([P, P], F32)
+        nc.scalar.copy(out=bias_rows[:], in_=bias_rows_bf[:])
+        bias_t = psum.tile([P, P], F32, tag="bank")
+        nc.tensor.transpose(bias_t[:], bias_rows[:], ident[:])
+        bias = const.tile([P, 2 * H_TILES], F32)
+        nc.scalar.mul(out=bias[:, 0:H_TILES], in_=bias_t[:, 0:H_TILES], mul=HALF_OVER_SQRT_D)
+        nc.scalar.copy(out=bias[:, H_TILES : 2 * H_TILES], in_=bias_t[:, H_TILES : 2 * H_TILES])
+        out_scale = [HALF_OVER_SQRT_D, 1.0]
+
+        w_codes = const.tile([P, 2, D_PASSES, H], U32, align_bytes=64)
+        w_scales = const.tile([P, 2, D_PASSES, H], U8, align_bytes=64)
+
+        def regroup(dst, src):
+            nc.vector.tensor_copy(
+                out=dst.rearrange("p (c i t) -> p c t i", i=4, t=PACK),
+                in_=src.rearrange("p t (c i) -> p c t i", i=4),
+            )
+
+        def quantise_weight(w):
+            w_grouped = []
+            for g in range(D_PASSES):
+                w_grouped.append(w_stage.tile([P, PACK * H], BF16, align_bytes=64, name="w_grouped"))
+                regroup(w_grouped[g][:], w_raws[w][:, PACK * g : PACK * (g + 1), :])
+            for g in range(D_PASSES):
+                nc.vector.quantize_mx(
+                    out=w_codes[:, w, g, :].bitcast(FP8X4), scales=w_scales[:, w, g, :], in_=w_grouped[g][:]
+                )
+
+        def transpose_x(b):
+            x_grouped = x_mx.tile([P, D_PASSES, PACK * S], BF16, align_bytes=64, name="x_grouped")
+            for half in range(2):
+                for g in range(D_PASSES):
+                    xt = psum.tile([P, 2, 2 * P], F32, tag="bank", name="xt")
+                    for u in range(2):
+                        for rr in range(2):
+                            words = x_tiles[b][:, 2 * half + rr, :].bitcast(F32)
+                            first = (2 * g + u) * P
+                            nc.tensor.transpose(
+                                xt[:, u, rr * P : (rr + 1) * P], words[:, first : first + P], ident[:]
+                            )
+                    dst = x_grouped[:, g, half * 2 * K_PASS : (half + 1) * 2 * K_PASS]
+                    dst = dst.bitcast(F32).rearrange("p (s u) -> p s u", u=2)
+                    src = xt[:].rearrange("p u s -> p s u")
+                    if g == 0:
+                        nc.scalar.copy(out=dst, in_=src)
+                    else:
+                        nc.vector.tensor_copy(out=dst, in_=src)
+            return x_grouped
+
+        def quantise_x(x_grouped):
+            x_codes = x_mx.tile([P, D_PASSES, S], U32, align_bytes=64, name="x_codes")
+            x_scales = x_mx.tile([P, D_PASSES, S], U8, align_bytes=64, name="x_scales")
+            for g in range(D_PASSES):
+                nc.vector.quantize_mx(
+                    out=x_codes[:, g, :].bitcast(FP8X4), scales=x_scales[:, g, :], in_=x_grouped[:, g, :]
+                )
+            return x_codes, x_scales
+
+        def project(x_q, w, planes, m):
+            x_codes, x_scales = x_q
+            cols = slice(m * P, (m + 1) * P)
+            acc = psum.tile([P, S], F32, tag="bank", name="acc")
+            for g in range(D_PASSES):
+                nc.tensor.matmul_mx(
+                    out=acc[:],
+                    lhsT=w_codes[:, w, g, cols].bitcast(FP8X4),
+                    lhsT_scale=w_scales[:, w, g, cols],
+                    rhs=x_codes[:, g, :].bitcast(FP8X4),
+                    rhs_scale=x_scales[:, g, :],
+                    start=(g == 0),
+                    stop=(g == D_PASSES - 1),
+                )
+            nc.scalar.activation(
+                out=planes[:, m, :],
+                in_=acc[:],
+                func=ACT.Identity,
+                bias=bias[:, w * H_TILES + m : w * H_TILES + m + 1],
+                scale=out_scale[w],
+            )
+
+        def quantise_hidden(grouped):
+            codes = hid_mx.tile([P, S], U32, align_bytes=64, name="hid_codes")
+            scales = hid_mx.tile([P, S], U8, align_bytes=64, name="hid_scales")
+            nc.vector.quantize_mx(out=codes[:].bitcast(FP8X4), scales=scales[:], in_=grouped[:])
+            return codes, scales
+
+        def score_rows(b, phi_q, theta_q, i):
+            rows = slice(i * P, (i + 1) * P)
+            banks = []
+            for stationary, moving in ((phi_q, theta_q), (theta_q, phi_q)):
+                prod = psum.tile([P, S], F32, tag="bank", name="prod")
+                nc.tensor.matmul_mx(
+                    out=prod[:],
+                    lhsT=stationary[0][:, rows].bitcast(FP8X4),
+                    lhsT_scale=stationary[1][:, rows],
+                    rhs=moving[0][:].bitcast(FP8X4),
+                    rhs_scale=moving[1][:],
+                    start=True,
+                    stop=True,
+                )
+                banks.append(prod)
+            relu_a = ends.tile([P, S], F32, name="relu_a")
+            nc.scalar.activation(out=relu_a[:], in_=banks[0][:], func=ACT.Relu)
+            result = ends.tile([P, S], F32, name="result")
+            nc.vector.scalar_tensor_tensor(
+                out=result[:], in0=banks[1][:], scalar=0.0, in1=relu_a[:], op0=ALU.max, op1=ALU.add
+            )
+            nc.sync.dma_start(out=out[b, rows, :], in_=result[:])
+
+        quantise_weight(PHI)
+        x_q = {0: quantise_x(transpose_x(0))}
+        quantise_weight(THETA)
+        hid_q = {}
+        waiting = None
+        x_grouped = None
+        for step in range(2 * B + SCORE_LAG):
+            b, w = divmod(step, 2)
+            scored, rows_half = divmod(step - SCORE_LAG, 2)
+            if waiting is not None:
+                hid_q[waiting[0], waiting[1]] = quantise_hidden(waiting[2])
+                waiting = None
+            if x_grouped is not None:
+                x_q[b + 1] = quantise_x(x_grouped)
+                x_grouped = None
+            if b < B:
+                planes = hid.tile([P, H_TILES, S], BF16, name="planes")
+            for j in range(2):
+                if b < B:
+                    project(x_q[b], w, planes, 2 * j)
+                if scored >= 0:
+                    score_rows(scored, hid_q[scored, PHI], hid_q[scored, THETA], 2 * rows_half + j)
+                if b < B:
+                    project(x_q[b], w, planes, 2 * j + 1)
+            if w == PHI and b + 1 < B:
+                x_grouped = transpose_x(b + 1)
+            if b < B:
+                grouped = hid.tile([P, PACK * S], BF16, align_bytes=64, name="grouped")
+                regroup(grouped[:], planes[:])
+                waiting = (b, w, grouped)

@@ -45,8 +45,8 @@ def tile_selfattention_pa_t_kernel(tc, audio_feature, W_phi, b_phi, W_theta, b_t
 
         bias_rows_bf = const.tile([P, P], BF16)
         nc.vector.memset(bias_rows_bf[:], 0.0)
-        nc.scalar.dma_start(out=bias_rows_bf[0:H_TILES, :], in_=b_phi.rearrange("(m p) -> m p", p=P))
-        nc.scalar.dma_start(
+        nc.sync.dma_start(out=bias_rows_bf[0:H_TILES, :], in_=b_phi.rearrange("(m p) -> m p", p=P))
+        nc.sync.dma_start(
             out=bias_rows_bf[H_TILES : 2 * H_TILES, :], in_=b_theta.rearrange("(m p) -> m p", p=P)
         )
 
@@ -75,13 +75,16 @@ def tile_selfattention_pa_t_kernel(tc, audio_feature, W_phi, b_phi, W_theta, b_t
         ident = const.tile([P, P], F32)
         make_identity(nc, ident[:])
 
-        bias_rows = const.tile([P, P], F32)
-        nc.scalar.copy(out=bias_rows[:], in_=bias_rows_bf[:])
-        bias_t = psum.tile([P, P], F32, tag="bank")
-        nc.tensor.transpose(bias_t[:], bias_rows[:], ident[:])
         bias = const.tile([P, 2 * H_TILES], F32)
-        nc.scalar.mul(out=bias[:, 0:H_TILES], in_=bias_t[:, 0:H_TILES], mul=HALF_OVER_SQRT_D)
-        nc.scalar.copy(out=bias[:, H_TILES : 2 * H_TILES], in_=bias_t[:, H_TILES : 2 * H_TILES])
+
+        def spread_biases():
+            bias_rows = const.tile([P, P], F32)
+            nc.scalar.copy(out=bias_rows[:], in_=bias_rows_bf[:])
+            bias_t = psum.tile([P, P], F32, tag="bank")
+            nc.tensor.transpose(bias_t[:], bias_rows[:], ident[:])
+            nc.scalar.mul(out=bias[:, 0:H_TILES], in_=bias_t[:, 0:H_TILES], mul=HALF_OVER_SQRT_D)
+            nc.scalar.copy(out=bias[:, H_TILES : 2 * H_TILES], in_=bias_t[:, H_TILES : 2 * H_TILES])
+
         out_scale = [HALF_OVER_SQRT_D, 1.0]
 
         w_codes = const.tile([P, 2, D_PASSES, H], U32, align_bytes=64)
@@ -186,6 +189,7 @@ def tile_selfattention_pa_t_kernel(tc, audio_feature, W_phi, b_phi, W_theta, b_t
 
         quantise_weight(PHI)
         x_q = {0: quantise_x(transpose_x(0))}
+        spread_biases()
         quantise_weight(THETA)
         hid_q = {}
         waiting = None
@@ -193,24 +197,24 @@ def tile_selfattention_pa_t_kernel(tc, audio_feature, W_phi, b_phi, W_theta, b_t
         for step in range(2 * B + SCORE_LAG):
             b, w = divmod(step, 2)
             scored, rows_half = divmod(step - SCORE_LAG, 2)
-            if waiting is not None:
-                hid_q[waiting[0], waiting[1]] = quantise_hidden(waiting[2])
-                waiting = None
             if x_grouped is not None:
                 x_q[b + 1] = quantise_x(x_grouped)
                 x_grouped = None
+            if waiting is not None:
+                hid_q[waiting[0], waiting[1]] = quantise_hidden(waiting[2])
+                waiting = None
             if b < B:
                 planes = hid.tile([P, H_TILES, S], BF16, name="planes")
-            for j in range(2):
-                if b < B:
-                    project(x_q[b], w, planes, 2 * j)
-                if scored >= 0:
-                    score_rows(scored, hid_q[scored, PHI], hid_q[scored, THETA], 2 * rows_half + j)
-                if b < B:
-                    project(x_q[b], w, planes, 2 * j + 1)
-            if w == PHI and b + 1 < B:
-                x_grouped = transpose_x(b + 1)
+                project(x_q[b], w, planes, 0)
+            if scored >= 0:
+                score_rows(scored, hid_q[scored, PHI], hid_q[scored, THETA], 2 * rows_half)
             if b < B:
+                for m in range(1, H_TILES):
+                    project(x_q[b], w, planes, m)
                 grouped = hid.tile([P, PACK * S], BF16, align_bytes=64, name="grouped")
                 regroup(grouped[:], planes[:])
                 waiting = (b, w, grouped)
+            if scored >= 0:
+                score_rows(scored, hid_q[scored, PHI], hid_q[scored, THETA], 2 * rows_half + 1)
+            if w == PHI and b + 1 < B:
+                x_grouped = transpose_x(b + 1)

@@ -40,7 +40,8 @@ def tile_selfattention_pa_t_kernel(tc, audio_feature, W_phi, b_phi, W_theta, b_t
         hid = ctx.enter_context(tc.tile_pool(name="hid", bufs=3))
         hid_mx = ctx.enter_context(tc.tile_pool(name="hid_mx", bufs=6))
         ends = ctx.enter_context(tc.tile_pool(name="ends", bufs=6))
-        psum = ctx.enter_context(tc.psum_pool(name="psum", bufs=8))
+        psum_s = ctx.enter_context(tc.psum_pool(name="psum_s", bufs=4))
+        psum_v = ctx.enter_context(tc.psum_pool(name="psum_v", bufs=4))
         ctx.enter_context(tc.manual_schedule())
 
         bias_rows_bf = const.tile([P, P], BF16)
@@ -80,7 +81,7 @@ def tile_selfattention_pa_t_kernel(tc, audio_feature, W_phi, b_phi, W_theta, b_t
         def spread_biases():
             bias_rows = const.tile([P, P], F32)
             nc.scalar.copy(out=bias_rows[:], in_=bias_rows_bf[:])
-            bias_t = psum.tile([P, P], F32, tag="bank")
+            bias_t = psum_s.tile([P, P], F32, tag="bank")
             nc.tensor.transpose(bias_t[:], bias_rows[:], ident[:])
             nc.scalar.mul(out=bias[:, 0:H_TILES], in_=bias_t[:, 0:H_TILES], mul=HALF_OVER_SQRT_D)
             nc.scalar.copy(out=bias[:, H_TILES : 2 * H_TILES], in_=bias_t[:, H_TILES : 2 * H_TILES])
@@ -110,7 +111,7 @@ def tile_selfattention_pa_t_kernel(tc, audio_feature, W_phi, b_phi, W_theta, b_t
             x_grouped = x_mx.tile([P, D_PASSES, PACK * S], BF16, align_bytes=64, name="x_grouped")
             for half in range(2):
                 for g in range(D_PASSES):
-                    xt = psum.tile([P, 2, 2 * P], F32, tag="bank", name="xt")
+                    xt = (psum_s if g == 0 else psum_v).tile([P, 2, 2 * P], F32, tag="bank", name="xt")
                     for u in range(2):
                         for rr in range(2):
                             words = x_tiles[b][:, 2 * half + rr, :].bitcast(F32)
@@ -139,7 +140,7 @@ def tile_selfattention_pa_t_kernel(tc, audio_feature, W_phi, b_phi, W_theta, b_t
         def project(x_q, w, planes, m):
             x_codes, x_scales = x_q
             cols = slice(m * P, (m + 1) * P)
-            acc = psum.tile([P, S], F32, tag="bank", name="acc")
+            acc = psum_s.tile([P, S], F32, tag="bank", name="acc")
             for g in range(D_PASSES):
                 nc.tensor.matmul_mx(
                     out=acc[:],
@@ -167,8 +168,8 @@ def tile_selfattention_pa_t_kernel(tc, audio_feature, W_phi, b_phi, W_theta, b_t
         def score_rows(b, phi_q, theta_q, i):
             rows = slice(i * P, (i + 1) * P)
             banks = []
-            for stationary, moving in ((phi_q, theta_q), (theta_q, phi_q)):
-                prod = psum.tile([P, S], F32, tag="bank", name="prod")
+            for stationary, moving, pool in ((phi_q, theta_q, psum_s), (theta_q, phi_q, psum_v)):
+                prod = pool.tile([P, S], F32, tag="bank", name="prod")
                 nc.tensor.matmul_mx(
                     out=prod[:],
                     lhsT=stationary[0][:, rows].bitcast(FP8X4),
@@ -193,28 +194,29 @@ def tile_selfattention_pa_t_kernel(tc, audio_feature, W_phi, b_phi, W_theta, b_t
         quantise_weight(THETA)
         hid_q = {}
         waiting = None
-        x_grouped = None
         for step in range(2 * B + SCORE_LAG):
             b, w = divmod(step, 2)
             scored, rows_half = divmod(step - SCORE_LAG, 2)
-            if x_grouped is not None:
-                x_q[b + 1] = quantise_x(x_grouped)
-                x_grouped = None
-            if waiting is not None:
-                hid_q[waiting[0], waiting[1]] = quantise_hidden(waiting[2])
-                waiting = None
+            x_grouped = None
             if b < B:
                 planes = hid.tile([P, H_TILES, S], BF16, name="planes")
                 project(x_q[b], w, planes, 0)
+                project(x_q[b], w, planes, 1)
+            if w == PHI and b + 1 < B:
+                x_grouped = transpose_x(b + 1)
+            if waiting is not None:
+                hid_q[waiting[0], waiting[1]] = quantise_hidden(waiting[2])
+                waiting = None
+            if x_grouped is not None:
+                x_q[b + 1] = quantise_x(x_grouped)
+            if b < B:
+                project(x_q[b], w, planes, 2)
             if scored >= 0:
                 score_rows(scored, hid_q[scored, PHI], hid_q[scored, THETA], 2 * rows_half)
             if b < B:
-                for m in range(1, H_TILES):
-                    project(x_q[b], w, planes, m)
+                project(x_q[b], w, planes, 3)
                 grouped = hid.tile([P, PACK * S], BF16, align_bytes=64, name="grouped")
                 regroup(grouped[:], planes[:])
                 waiting = (b, w, grouped)
             if scored >= 0:
                 score_rows(scored, hid_q[scored, PHI], hid_q[scored, THETA], 2 * rows_half + 1)
-            if w == PHI and b + 1 < B:
-                x_grouped = transpose_x(b + 1)

@@ -19,6 +19,7 @@ K_PASS = P * PACK
 B, S, D, H = 8, 512, 1024, 512
 D_PASSES = D // K_PASS
 ROW_TILES = S // P
+HALF = S // 2
 H_TILES = H // P
 assert H_TILES == PACK
 PHI, THETA = 0, 1
@@ -27,6 +28,7 @@ HALF_OVER_SQRT_D = 0.5 / math.sqrt(D)
 FLOPS = 2 * B * S * D * (2 * H) + 2 * B * S * S * H
 
 
+WEIGHT_SPLIT = 336
 SCORE_LAG = 3
 
 
@@ -39,7 +41,12 @@ def tile_selfattention_pa_t_kernel(tc, audio_feature, W_phi, b_phi, W_theta, b_t
         x_mx = ctx.enter_context(tc.tile_pool(name="x_mx", bufs=2))
         hid = ctx.enter_context(tc.tile_pool(name="hid", bufs=3))
         hid_mx = ctx.enter_context(tc.tile_pool(name="hid_mx", bufs=6))
-        ends = ctx.enter_context(tc.tile_pool(name="ends", bufs=6))
+        ends = ctx.enter_context(tc.tile_pool(name="ends", bufs=4))
+        tops = ctx.enter_context(tc.tile_pool(name="tops", bufs=8))
+        bottoms = ctx.enter_context(tc.tile_pool(name="bottoms", bufs=3))
+        warm = const.tile([P, 1], F32)
+        nc.vector.memset(warm[:], 0.0)
+        nc.scalar.activation(out=warm[:], in_=warm[:], func=ACT.Relu)
         psum_s = ctx.enter_context(tc.psum_pool(name="psum_s", bufs=4))
         psum_v = ctx.enter_context(tc.psum_pool(name="psum_v", bufs=4))
         ctx.enter_context(tc.manual_schedule())
@@ -91,27 +98,33 @@ def tile_selfattention_pa_t_kernel(tc, audio_feature, W_phi, b_phi, W_theta, b_t
         w_codes = const.tile([P, 2, D_PASSES, H], U32, align_bytes=64)
         w_scales = const.tile([P, 2, D_PASSES, H], U8, align_bytes=64)
 
-        def regroup(dst, src):
-            nc.vector.tensor_copy(
-                out=dst.rearrange("p (c i t) -> p c t i", i=4, t=PACK),
-                in_=src.rearrange("p t (c i) -> p c t i", i=4),
-            )
+        def regroup(dst, src, split):
+            def view(first, last):
+                return dict(
+                    out=dst[:, PACK * first : PACK * last].rearrange("p (c i t) -> p c t i", i=4, t=PACK),
+                    in_=src[:, :, first:last].rearrange("p t (c i) -> p c t i", i=4),
+                )
+
+            nc.vector.tensor_copy(**view(0, split))
+            if split < S:
+                nc.scalar.copy(**view(split, S))
 
         def quantise_weight(w):
             w_grouped = []
             for g in range(D_PASSES):
                 w_grouped.append(w_stage.tile([P, PACK * H], BF16, align_bytes=64, name="w_grouped"))
-                regroup(w_grouped[g][:], w_raws[w][:, PACK * g : PACK * (g + 1), :])
+                regroup(w_grouped[g][:], w_raws[w][:, PACK * g : PACK * (g + 1), :], WEIGHT_SPLIT)
             for g in range(D_PASSES):
                 nc.vector.quantize_mx(
                     out=w_codes[:, w, g, :].bitcast(FP8X4), scales=w_scales[:, w, g, :], in_=w_grouped[g][:]
                 )
 
-        def transpose_x(b):
+        def transpose_x(b, then=None):
             x_grouped = x_mx.tile([P, D_PASSES, PACK * S], BF16, align_bytes=64, name="x_grouped")
             for half in range(2):
                 for g in range(D_PASSES):
-                    xt = (psum_s if g == 0 else psum_v).tile([P, 2, 2 * P], F32, tag="bank", name="xt")
+                    on_scalar = g == 0
+                    xt = (psum_s if on_scalar else psum_v).tile([P, 2, 2 * P], F32, tag="bank", name="xt")
                     for u in range(2):
                         for rr in range(2):
                             words = x_tiles[b][:, 2 * half + rr, :].bitcast(F32)
@@ -122,42 +135,52 @@ def tile_selfattention_pa_t_kernel(tc, audio_feature, W_phi, b_phi, W_theta, b_t
                     dst = x_grouped[:, g, half * 2 * K_PASS : (half + 1) * 2 * K_PASS]
                     dst = dst.bitcast(F32).rearrange("p (s u) -> p s u", u=2)
                     src = xt[:].rearrange("p u s -> p s u")
-                    if g == 0:
+                    if on_scalar:
                         nc.scalar.copy(out=dst, in_=src)
                     else:
                         nc.vector.tensor_copy(out=dst, in_=src)
+                if then is not None:
+                    then(x_grouped, half * HALF, HALF)
             return x_grouped
 
-        def quantise_x(x_grouped):
+        def new_x_q():
             x_codes = x_mx.tile([P, D_PASSES, S], U32, align_bytes=64, name="x_codes")
             x_scales = x_mx.tile([P, D_PASSES, S], U8, align_bytes=64, name="x_scales")
-            for g in range(D_PASSES):
-                nc.vector.quantize_mx(
-                    out=x_codes[:, g, :].bitcast(FP8X4), scales=x_scales[:, g, :], in_=x_grouped[:, g, :]
-                )
             return x_codes, x_scales
 
-        def project(x_q, w, planes, m):
-            x_codes, x_scales = x_q
-            cols = slice(m * P, (m + 1) * P)
-            acc = psum_s.tile([P, S], F32, tag="bank", name="acc")
+        def quantise_x(x_q, x_grouped, first=0, count=S):
             for g in range(D_PASSES):
-                nc.tensor.matmul_mx(
-                    out=acc[:],
-                    lhsT=w_codes[:, w, g, cols].bitcast(FP8X4),
-                    lhsT_scale=w_scales[:, w, g, cols],
-                    rhs=x_codes[:, g, :].bitcast(FP8X4),
-                    rhs_scale=x_scales[:, g, :],
-                    start=(g == 0),
-                    stop=(g == D_PASSES - 1),
+                nc.vector.quantize_mx(
+                    out=x_q[0][:, g, first : first + count].bitcast(FP8X4),
+                    scales=x_q[1][:, g, first : first + count],
+                    in_=x_grouped[:, g, PACK * first : PACK * (first + count)],
                 )
-            nc.scalar.activation(
-                out=planes[:, m, :],
-                in_=acc[:],
-                func=ACT.Identity,
-                bias=bias[:, w * H_TILES + m : w * H_TILES + m + 1],
-                scale=out_scale[w],
-            )
+
+        def project(x_q, w, planes, tiles, step=S):
+            x_codes, x_scales = x_q
+            accs = [psum_s.tile([P, S], F32, tag="bank", name="acc") for tile_m in tiles]
+            for first in range(0, S, step):
+                positions = slice(first, first + step)
+                for acc, m in zip(accs, tiles):
+                    cols = slice(m * P, (m + 1) * P)
+                    for g in range(D_PASSES):
+                        nc.tensor.matmul_mx(
+                            out=acc[:, positions],
+                            lhsT=w_codes[:, w, g, cols].bitcast(FP8X4),
+                            lhsT_scale=w_scales[:, w, g, cols],
+                            rhs=x_codes[:, g, positions].bitcast(FP8X4),
+                            rhs_scale=x_scales[:, g, positions],
+                            start=(g == 0),
+                            stop=(g == D_PASSES - 1),
+                        )
+            for acc, m in zip(accs, tiles):
+                nc.scalar.activation(
+                    out=planes[:, m, :],
+                    in_=acc[:],
+                    func=ACT.Identity,
+                    bias=bias[:, w * H_TILES + m : w * H_TILES + m + 1],
+                    scale=out_scale[w],
+                )
 
         def quantise_hidden(grouped):
             codes = hid_mx.tile([P, S], U32, align_bytes=64, name="hid_codes")
@@ -165,58 +188,132 @@ def tile_selfattention_pa_t_kernel(tc, audio_feature, W_phi, b_phi, W_theta, b_t
             nc.vector.quantize_mx(out=codes[:].bitcast(FP8X4), scales=scales[:], in_=grouped[:])
             return codes, scales
 
-        def score_rows(b, phi_q, theta_q, i):
+        def score_pass(dst, stationary, i, moving, first, count):
             rows = slice(i * P, (i + 1) * P)
-            banks = []
-            for stationary, moving, pool in ((phi_q, theta_q, psum_s), (theta_q, phi_q, psum_v)):
-                prod = pool.tile([P, S], F32, tag="bank", name="prod")
-                nc.tensor.matmul_mx(
-                    out=prod[:],
-                    lhsT=stationary[0][:, rows].bitcast(FP8X4),
-                    lhsT_scale=stationary[1][:, rows],
-                    rhs=moving[0][:].bitcast(FP8X4),
-                    rhs_scale=moving[1][:],
-                    start=True,
-                    stop=True,
-                )
-                banks.append(prod)
-            relu_a = ends.tile([P, S], F32, name="relu_a")
-            nc.scalar.activation(out=relu_a[:], in_=banks[0][:], func=ACT.Relu)
-            result = ends.tile([P, S], F32, name="result")
-            nc.vector.scalar_tensor_tensor(
-                out=result[:], in0=banks[1][:], scalar=0.0, in1=relu_a[:], op0=ALU.max, op1=ALU.add
+            cols = slice(first, first + count)
+            nc.tensor.matmul_mx(
+                out=dst,
+                lhsT=stationary[0][:, rows].bitcast(FP8X4),
+                lhsT_scale=stationary[1][:, rows],
+                rhs=moving[0][:, cols].bitcast(FP8X4),
+                rhs_scale=moving[1][:, cols],
+                start=True,
+                stop=True,
             )
-            nc.sync.dma_start(out=out[b, rows, :], in_=result[:])
 
-        quantise_weight(PHI)
-        x_q = {0: quantise_x(transpose_x(0))}
+        def relu_sum(dst, bank_s, bank_v):
+            relu_a = ends.tile(list(bank_s.shape), F32, tag="relu_a", name="relu_a")
+            nc.scalar.activation(out=relu_a[:], in_=bank_s, func=ACT.Relu)
+            nc.vector.scalar_tensor_tensor(
+                out=dst, in0=bank_v, scalar=0.0, in1=relu_a[:], op0=ALU.max, op1=ALU.add
+            )
+
+        def score_top(b, i):
+            bank_s = psum_s.tile([P, S], F32, tag="bank", name="prod_s")
+            bank_v = psum_v.tile([P, S], F32, tag="bank", name="prod_v")
+            score_pass(bank_s[:], hid_q[b, PHI], i, hid_q[b, THETA], 0, S)
+            score_pass(bank_v[:], hid_q[b, THETA], i, hid_q[b, PHI], 0, S)
+            top = tops.tile([P, S], F32, name="top")
+            relu_sum(top[:], bank_s[:], bank_v[:])
+            nc.sync.dma_start(out=out[b, i * P : (i + 1) * P, :], in_=top[:])
+            return top
+
+        def score_bottom(b, bottom):
+            bank_s = psum_s.tile([P, 2, HALF], F32, tag="bank", name="prod_s")
+            bank_v = psum_v.tile([P, 2, HALF], F32, tag="bank", name="prod_v")
+            for i in range(2):
+                score_pass(bank_s[:, i, :], hid_q[b, PHI], 2 + i, hid_q[b, THETA], HALF, HALF)
+            for i in range(2):
+                score_pass(bank_v[:, i, :], hid_q[b, THETA], 2 + i, hid_q[b, PHI], HALF, HALF)
+            relu_sum(bottom[:, :, HALF:S], bank_s[:], bank_v[:])
+
+        def mirror(bottom, tops_b):
+            bank = psum_s.tile([P, 2, HALF], F32, tag="bank", name="turned")
+            for i in range(2):
+                for j in range(2):
+                    nc.tensor.transpose(
+                        bank[:, i, j * P : (j + 1) * P],
+                        tops_b[j][:, HALF + i * P : HALF + (i + 1) * P],
+                        ident[:],
+                    )
+            nc.scalar.copy(out=bottom[:, :, 0:HALF], in_=bank[:])
+
+        def store_bottom(b, bottom):
+            nc.sync.dma_start(
+                out=out[b, HALF:S, :].rearrange("(i p) c -> p i c", p=P), in_=bottom[:]
+            )
+
         spread_biases()
+        quantise_weight(PHI)
+        x_q = {0: new_x_q()}
+        transpose_x(0, lambda grouped, first, count: quantise_x(x_q[0], grouped, first, count))
         quantise_weight(THETA)
         hid_q = {}
+        tops_of = {}
+        bottom_of = {}
         waiting = None
-        for step in range(2 * B + SCORE_LAG):
+        for step in range(2 * B - 1):
             b, w = divmod(step, 2)
-            scored, rows_half = divmod(step - SCORE_LAG, 2)
+            scored, part = divmod(step - SCORE_LAG, 2)
             x_grouped = None
             if b < B:
                 planes = hid.tile([P, H_TILES, S], BF16, name="planes")
-                project(x_q[b], w, planes, 0)
-                project(x_q[b], w, planes, 1)
+                if step == 0:
+                    project(x_q[b], w, planes, (0, 1, 2, 3), HALF)
+                else:
+                    project(x_q[b], w, planes, (0,))
+                    project(x_q[b], w, planes, (1,))
             if w == PHI and b + 1 < B:
                 x_grouped = transpose_x(b + 1)
+            if scored >= 0 and part == 1:
+                bottom_of[scored] = bottoms.tile([P, 2, S], F32, name="bottom")
+                if x_grouped is not None and scored > 0:
+                    mirror(bottom_of[scored - 1], tops_of[scored - 1])
+                    store_bottom(scored - 1, bottom_of[scored - 1])
             if waiting is not None:
                 hid_q[waiting[0], waiting[1]] = quantise_hidden(waiting[2])
                 waiting = None
             if x_grouped is not None:
-                x_q[b + 1] = quantise_x(x_grouped)
-            if b < B:
-                project(x_q[b], w, planes, 2)
+                x_q[b + 1] = new_x_q()
+                quantise_x(x_q[b + 1], x_grouped)
+            if step > 0:
+                project(x_q[b], w, planes, (2,))
             if scored >= 0:
-                score_rows(scored, hid_q[scored, PHI], hid_q[scored, THETA], 2 * rows_half)
+                if part == 0:
+                    tops_of[scored] = [score_top(scored, 0)]
+                else:
+                    score_bottom(scored, bottom_of[scored])
+                    if x_grouped is None:
+                        mirror(bottom_of[scored - 1], tops_of[scored - 1])
+                        store_bottom(scored - 1, bottom_of[scored - 1])
+            if step > 0:
+                project(x_q[b], w, planes, (3,))
             if b < B:
-                project(x_q[b], w, planes, 3)
                 grouped = hid.tile([P, PACK * S], BF16, align_bytes=64, name="grouped")
-                regroup(grouped[:], planes[:])
+                regroup(grouped[:], planes[:], S)
                 waiting = (b, w, grouped)
-            if scored >= 0:
-                score_rows(scored, hid_q[scored, PHI], hid_q[scored, THETA], 2 * rows_half + 1)
+            if scored >= 0 and part == 0:
+                tops_of[scored].append(score_top(scored, 1))
+
+        b = B - 1
+        planes = hid.tile([P, H_TILES, S], BF16, name="planes")
+        for m in range(H_TILES):
+            project(x_q[b], THETA, planes, (m,))
+        mirror(bottom_of[b - 2], tops_of[b - 2])
+        store_bottom(b - 2, bottom_of[b - 2])
+        hid_q[b, PHI] = quantise_hidden(waiting[2])
+        grouped = hid.tile([P, PACK * S], BF16, align_bytes=64, name="grouped")
+        regroup(grouped[:], planes[:], WEIGHT_SPLIT)
+        hid_q[b, THETA] = quantise_hidden(grouped)
+        top_0 = score_top(b - 1, 0)
+        top_1 = score_top(b - 1, 1)
+        bottom = bottoms.tile([P, 2, S], F32, name="bottom")
+        score_bottom(b - 1, bottom)
+        top_2 = score_top(b, 0)
+        top_3 = score_top(b, 1)
+        mirror(bottom, [top_0, top_1])
+        store_bottom(b - 1, bottom)
+        bottom = bottoms.tile([P, 2, S], F32, name="bottom")
+        score_bottom(b, bottom)
+        mirror(bottom, [top_2, top_3])
+        store_bottom(b, bottom)

@@ -95,8 +95,8 @@ def tile_selfattention_pa_t_kernel(tc, audio_feature, W_phi, b_phi, W_theta, b_t
 
         out_scale = [HALF_OVER_SQRT_D, 1.0]
 
-        w_codes = const.tile([P, 2, D_PASSES, H], U32, align_bytes=64)
-        w_scales = const.tile([P, 2, D_PASSES, H], U8, align_bytes=64)
+        w_codes = const.tile([P, 2, D_PASSES, H], U32, align_bytes=256)
+        w_scales = const.tile([P, 2, D_PASSES, H], U8, align_bytes=256)
 
         def regroup(dst, src, split):
             def view(first, last):
@@ -112,7 +112,7 @@ def tile_selfattention_pa_t_kernel(tc, audio_feature, W_phi, b_phi, W_theta, b_t
         def quantise_weight(w):
             w_grouped = []
             for g in range(D_PASSES):
-                w_grouped.append(w_stage.tile([P, PACK * H], BF16, align_bytes=64, name="w_grouped"))
+                w_grouped.append(w_stage.tile([P, PACK * H], BF16, align_bytes=256, name="w_grouped"))
                 regroup(w_grouped[g][:], w_raws[w][:, PACK * g : PACK * (g + 1), :], WEIGHT_SPLIT)
             for g in range(D_PASSES):
                 nc.vector.quantize_mx(
@@ -120,7 +120,7 @@ def tile_selfattention_pa_t_kernel(tc, audio_feature, W_phi, b_phi, W_theta, b_t
                 )
 
         def transpose_x(b, then=None):
-            x_grouped = x_mx.tile([P, D_PASSES, PACK * S], BF16, align_bytes=64, name="x_grouped")
+            x_grouped = x_mx.tile([P, D_PASSES, PACK * S], BF16, align_bytes=256, name="x_grouped")
             for half in range(2):
                 for g in range(D_PASSES):
                     on_scalar = g == 0
@@ -144,8 +144,8 @@ def tile_selfattention_pa_t_kernel(tc, audio_feature, W_phi, b_phi, W_theta, b_t
             return x_grouped
 
         def new_x_q():
-            x_codes = x_mx.tile([P, D_PASSES, S], U32, align_bytes=64, name="x_codes")
-            x_scales = x_mx.tile([P, D_PASSES, S], U8, align_bytes=64, name="x_scales")
+            x_codes = x_mx.tile([P, D_PASSES, S], U32, align_bytes=256, name="x_codes")
+            x_scales = x_mx.tile([P, D_PASSES, S], U8, align_bytes=256, name="x_scales")
             return x_codes, x_scales
 
         def quantise_x(x_q, x_grouped, first=0, count=S):
@@ -183,8 +183,8 @@ def tile_selfattention_pa_t_kernel(tc, audio_feature, W_phi, b_phi, W_theta, b_t
                 )
 
         def quantise_hidden(grouped):
-            codes = hid_mx.tile([P, S], U32, align_bytes=64, name="hid_codes")
-            scales = hid_mx.tile([P, S], U8, align_bytes=64, name="hid_scales")
+            codes = hid_mx.tile([P, S], U32, align_bytes=256, name="hid_codes")
+            scales = hid_mx.tile([P, S], U8, align_bytes=256, name="hid_scales")
             nc.vector.quantize_mx(out=codes[:].bitcast(FP8X4), scales=scales[:], in_=grouped[:])
             return codes, scales
 
@@ -289,7 +289,7 @@ def tile_selfattention_pa_t_kernel(tc, audio_feature, W_phi, b_phi, W_theta, b_t
             if step > 0:
                 project(x_q[b], w, planes, (3,))
             if b < B:
-                grouped = hid.tile([P, PACK * S], BF16, align_bytes=64, name="grouped")
+                grouped = hid.tile([P, PACK * S], BF16, align_bytes=256, name="grouped")
                 regroup(grouped[:], planes[:], S)
                 waiting = (b, w, grouped)
             if scored >= 0 and part == 0:
@@ -302,7 +302,7 @@ def tile_selfattention_pa_t_kernel(tc, audio_feature, W_phi, b_phi, W_theta, b_t
         mirror(bottom_of[b - 2], tops_of[b - 2])
         store_bottom(b - 2, bottom_of[b - 2])
         hid_q[b, PHI] = quantise_hidden(waiting[2])
-        grouped = hid.tile([P, PACK * S], BF16, align_bytes=64, name="grouped")
+        grouped = hid.tile([P, PACK * S], BF16, align_bytes=256, name="grouped")
         regroup(grouped[:], planes[:], WEIGHT_SPLIT)
         hid_q[b, THETA] = quantise_hidden(grouped)
         top_0 = score_top(b - 1, 0)

@@ -29,6 +29,7 @@ FLOPS = 2 * B * S * D * (2 * H) + 2 * B * S * S * H
 
 
 WEIGHT_SPLIT = 336
+THETA_SPLIT = 208
 SCORE_LAG = 3
 
 
@@ -42,8 +43,8 @@ def tile_selfattention_pa_t_kernel(tc, audio_feature, W_phi, b_phi, W_theta, b_t
         hid = ctx.enter_context(tc.tile_pool(name="hid", bufs=3))
         hid_mx = ctx.enter_context(tc.tile_pool(name="hid_mx", bufs=6))
         ends = ctx.enter_context(tc.tile_pool(name="ends", bufs=4))
-        tops = ctx.enter_context(tc.tile_pool(name="tops", bufs=8))
-        bottoms = ctx.enter_context(tc.tile_pool(name="bottoms", bufs=3))
+        tops = ctx.enter_context(tc.tile_pool(name="tops", bufs=4))
+        lows = ctx.enter_context(tc.tile_pool(name="lows", bufs=3))
         warm = const.tile([P, 1], F32)
         nc.vector.memset(warm[:], 0.0)
         nc.scalar.activation(out=warm[:], in_=warm[:], func=ACT.Relu)
@@ -53,8 +54,8 @@ def tile_selfattention_pa_t_kernel(tc, audio_feature, W_phi, b_phi, W_theta, b_t
 
         bias_rows_bf = const.tile([P, P], BF16)
         nc.vector.memset(bias_rows_bf[:], 0.0)
-        nc.sync.dma_start(out=bias_rows_bf[0:H_TILES, :], in_=b_phi.rearrange("(m p) -> m p", p=P))
-        nc.sync.dma_start(
+        nc.scalar.dma_start(out=bias_rows_bf[0:H_TILES, :], in_=b_phi.rearrange("(m p) -> m p", p=P))
+        nc.scalar.dma_start(
             out=bias_rows_bf[H_TILES : 2 * H_TILES, :], in_=b_theta.rearrange("(m p) -> m p", p=P)
         )
 
@@ -106,8 +107,8 @@ def tile_selfattention_pa_t_kernel(tc, audio_feature, W_phi, b_phi, W_theta, b_t
                 )
 
             nc.vector.tensor_copy(**view(0, split))
-            if split < S:
-                nc.scalar.copy(**view(split, S))
+            if split < src.shape[2]:
+                nc.scalar.copy(**view(split, src.shape[2]))
 
         def quantise_weight(w):
             w_grouped = []
@@ -156,7 +157,7 @@ def tile_selfattention_pa_t_kernel(tc, audio_feature, W_phi, b_phi, W_theta, b_t
                     in_=x_grouped[:, g, PACK * first : PACK * (first + count)],
                 )
 
-        def project(x_q, w, planes, tiles, step=S):
+        def project(x_q, w, planes, tiles, step=S, split_out=False):
             x_codes, x_scales = x_q
             accs = [psum_s.tile([P, S], F32, tag="bank", name="acc") for tile_m in tiles]
             for first in range(0, S, step):
@@ -173,20 +174,33 @@ def tile_selfattention_pa_t_kernel(tc, audio_feature, W_phi, b_phi, W_theta, b_t
                             start=(g == 0),
                             stop=(g == D_PASSES - 1),
                         )
-            for acc, m in zip(accs, tiles):
-                nc.scalar.activation(
-                    out=planes[:, m, :],
-                    in_=acc[:],
-                    func=ACT.Identity,
-                    bias=bias[:, w * H_TILES + m : w * H_TILES + m + 1],
-                    scale=out_scale[w],
-                )
+                if split_out or first + step == S:
+                    done_positions = positions if split_out else slice(0, S)
+                    for acc, m in zip(accs, tiles):
+                        nc.scalar.activation(
+                            out=planes[:, m, done_positions],
+                            in_=acc[:, done_positions],
+                            func=ACT.Identity,
+                            bias=bias[:, w * H_TILES + m : w * H_TILES + m + 1],
+                            scale=out_scale[w],
+                        )
 
-        def quantise_hidden(grouped):
+        def new_hidden():
             codes = hid_mx.tile([P, S], U32, align_bytes=256, name="hid_codes")
             scales = hid_mx.tile([P, S], U8, align_bytes=256, name="hid_scales")
-            nc.vector.quantize_mx(out=codes[:].bitcast(FP8X4), scales=scales[:], in_=grouped[:])
             return codes, scales
+
+        def quantise_part(hidden, grouped, positions):
+            nc.vector.quantize_mx(
+                out=hidden[0][:, positions].bitcast(FP8X4),
+                scales=hidden[1][:, positions],
+                in_=grouped[:, PACK * positions.start : PACK * positions.stop],
+            )
+
+        def quantise_hidden(grouped):
+            hidden = new_hidden()
+            quantise_part(hidden, grouped, slice(0, S))
+            return hidden
 
         def score_pass(dst, stationary, i, moving, first, count):
             rows = slice(i * P, (i + 1) * P)
@@ -208,40 +222,53 @@ def tile_selfattention_pa_t_kernel(tc, audio_feature, W_phi, b_phi, W_theta, b_t
                 out=dst, in0=bank_v, scalar=0.0, in1=relu_a[:], op0=ALU.max, op1=ALU.add
             )
 
-        def score_top(b, i):
+        def score_row0(b):
             bank_s = psum_s.tile([P, S], F32, tag="bank", name="prod_s")
             bank_v = psum_v.tile([P, S], F32, tag="bank", name="prod_v")
-            score_pass(bank_s[:], hid_q[b, PHI], i, hid_q[b, THETA], 0, S)
-            score_pass(bank_v[:], hid_q[b, THETA], i, hid_q[b, PHI], 0, S)
-            top = tops.tile([P, S], F32, name="top")
-            relu_sum(top[:], bank_s[:], bank_v[:])
-            nc.sync.dma_start(out=out[b, i * P : (i + 1) * P, :], in_=top[:])
-            return top
+            score_pass(bank_s[:], hid_q[b, PHI], 0, hid_q[b, THETA], 0, S)
+            score_pass(bank_v[:], hid_q[b, THETA], 0, hid_q[b, PHI], 0, S)
+            r0 = tops.tile([P, S], F32, name="r0")
+            relu_sum(r0[:], bank_s[:], bank_v[:])
+            nc.sync.dma_start(out=out[b, 0:P, :], in_=r0[:])
+            return r0
 
-        def score_bottom(b, bottom):
-            bank_s = psum_s.tile([P, 2, HALF], F32, tag="bank", name="prod_s")
-            bank_v = psum_v.tile([P, 2, HALF], F32, tag="bank", name="prod_v")
-            for i in range(2):
-                score_pass(bank_s[:, i, :], hid_q[b, PHI], 2 + i, hid_q[b, THETA], HALF, HALF)
-            for i in range(2):
-                score_pass(bank_v[:, i, :], hid_q[b, THETA], 2 + i, hid_q[b, PHI], HALF, HALF)
-            relu_sum(bottom[:, :, HALF:S], bank_s[:], bank_v[:])
+        def score_rows13(b):
+            bank_s = psum_s.tile([P, S], F32, tag="bank", name="prod_s")
+            bank_v = psum_v.tile([P, S], F32, tag="bank", name="prod_v")
+            for bank, stationary, moving in ((bank_s, PHI, THETA), (bank_v, THETA, PHI)):
+                score_pass(bank[:, 0:HALF], hid_q[b, stationary], 1, hid_q[b, moving], P, HALF)
+                score_pass(bank[:, HALF : 3 * P], hid_q[b, stationary], 1, hid_q[b, moving], 3 * P, P)
+                score_pass(bank[:, 3 * P : S], hid_q[b, stationary], 3, hid_q[b, moving], 3 * P, P)
+            r13 = tops.tile([P, S], F32, name="r13")
+            relu_sum(r13[:], bank_s[:], bank_v[:])
+            nc.sync.dma_start(out=out[b, P : 2 * P, P:S], in_=r13[:, 0 : 3 * P])
+            nc.sync.dma_start(out=out[b, 3 * P : S, 3 * P : S], in_=r13[:, 3 * P : S])
+            return r13
 
-        def mirror(bottom, tops_b):
-            bank = psum_s.tile([P, 2, HALF], F32, tag="bank", name="turned")
-            for i in range(2):
-                for j in range(2):
-                    nc.tensor.transpose(
-                        bank[:, i, j * P : (j + 1) * P],
-                        tops_b[j][:, HALF + i * P : HALF + (i + 1) * P],
-                        ident[:],
-                    )
-            nc.scalar.copy(out=bottom[:, :, 0:HALF], in_=bank[:])
+        def score_row2(b):
+            bank_s = psum_s.tile([P, S], F32, tag="bank", name="prod_s")
+            bank_v = psum_v.tile([P, S], F32, tag="bank", name="prod_v")
+            score_pass(bank_s[:, 0:HALF], hid_q[b, PHI], 2, hid_q[b, THETA], HALF, HALF)
+            score_pass(bank_v[:, 0:HALF], hid_q[b, THETA], 2, hid_q[b, PHI], HALF, HALF)
+            r2 = tops.tile([P, HALF], F32, name="r2")
+            relu_sum(r2[:], bank_s[:, 0:HALF], bank_v[:, 0:HALF])
+            nc.sync.dma_start(out=out[b, HALF : HALF + P, HALF:S], in_=r2[:])
+            return r2
 
-        def store_bottom(b, bottom):
-            nc.sync.dma_start(
-                out=out[b, HALF:S, :].rearrange("(i p) c -> p i c", p=P), in_=bottom[:]
-            )
+        def mirror(b, r0, r13, r2):
+            low21 = lows.tile([P, 3 * P], F32, name="low21")
+            low3 = lows.tile([P, 3 * P], F32, name="low3")
+            for low, blocks in (
+                (low21, (r0[:, 2 * P : 3 * P], r13[:, P : 2 * P], r0[:, P : 2 * P])),
+                (low3, (r0[:, 3 * P : S], r13[:, 2 * P : 3 * P], r2[:, P : 2 * P])),
+            ):
+                bank = psum_s.tile([P, S], F32, tag="bank", name="turned")
+                for i, block in enumerate(blocks):
+                    nc.tensor.transpose(bank[:, i * P : (i + 1) * P], block, ident[:])
+                nc.scalar.copy(out=low[:], in_=bank[:, 0 : 3 * P])
+            nc.sync.dma_start(out=out[b, HALF : HALF + P, 0:HALF], in_=low21[:, 0:HALF])
+            nc.sync.dma_start(out=out[b, P : 2 * P, 0:P], in_=low21[:, HALF : 3 * P])
+            nc.sync.dma_start(out=out[b, 3 * P : S, 0 : 3 * P], in_=low3[:])
 
         spread_biases()
         quantise_weight(PHI)
@@ -249,28 +276,23 @@ def tile_selfattention_pa_t_kernel(tc, audio_feature, W_phi, b_phi, W_theta, b_t
         transpose_x(0, lambda grouped, first, count: quantise_x(x_q[0], grouped, first, count))
         quantise_weight(THETA)
         hid_q = {}
-        tops_of = {}
-        bottom_of = {}
+        done = {}
         waiting = None
         for step in range(2 * B - 1):
             b, w = divmod(step, 2)
             scored, part = divmod(step - SCORE_LAG, 2)
             x_grouped = None
-            if b < B:
-                planes = hid.tile([P, H_TILES, S], BF16, name="planes")
-                if step == 0:
-                    project(x_q[b], w, planes, (0, 1, 2, 3), HALF)
-                else:
-                    project(x_q[b], w, planes, (0,))
-                    project(x_q[b], w, planes, (1,))
+            planes = hid.tile([P, H_TILES, S], BF16, name="planes")
+            if step == 0:
+                project(x_q[b], w, planes, (0, 1, 2, 3), HALF)
+            else:
+                project(x_q[b], w, planes, (0,))
+                project(x_q[b], w, planes, (1,))
             if w == PHI and b + 1 < B:
                 x_grouped = transpose_x(b + 1)
-            if scored >= 0 and part == 1:
-                bottom_of[scored] = bottoms.tile([P, 2, S], F32, name="bottom")
-                if x_grouped is not None and scored > 0:
-                    mirror(bottom_of[scored - 1], tops_of[scored - 1])
-                    store_bottom(scored - 1, bottom_of[scored - 1])
-            if waiting is not None:
+                if scored > 0:
+                    mirror(scored - 1, *done[scored - 1])
+            if waiting is not None and w == PHI:
                 hid_q[waiting[0], waiting[1]] = quantise_hidden(waiting[2])
                 waiting = None
             if x_grouped is not None:
@@ -280,40 +302,36 @@ def tile_selfattention_pa_t_kernel(tc, audio_feature, W_phi, b_phi, W_theta, b_t
                 project(x_q[b], w, planes, (2,))
             if scored >= 0:
                 if part == 0:
-                    tops_of[scored] = [score_top(scored, 0)]
+                    done[scored] = [score_row0(scored)]
                 else:
-                    score_bottom(scored, bottom_of[scored])
+                    done[scored].append(score_row2(scored))
                     if x_grouped is None:
-                        mirror(bottom_of[scored - 1], tops_of[scored - 1])
-                        store_bottom(scored - 1, bottom_of[scored - 1])
+                        mirror(scored - 1, *done[scored - 1])
+            if waiting is not None:
+                hid_q[waiting[0], waiting[1]] = quantise_hidden(waiting[2])
+                waiting = None
             if step > 0:
                 project(x_q[b], w, planes, (3,))
-            if b < B:
-                grouped = hid.tile([P, PACK * S], BF16, align_bytes=256, name="grouped")
-                regroup(grouped[:], planes[:], S)
-                waiting = (b, w, grouped)
+            grouped = hid.tile([P, PACK * S], BF16, align_bytes=256, name="grouped")
+            regroup(grouped[:], planes[:], S)
+            waiting = (b, w, grouped)
             if scored >= 0 and part == 0:
-                tops_of[scored].append(score_top(scored, 1))
+                done[scored].append(score_rows13(scored))
 
         b = B - 1
         planes = hid.tile([P, H_TILES, S], BF16, name="planes")
-        for m in range(H_TILES):
-            project(x_q[b], THETA, planes, (m,))
-        mirror(bottom_of[b - 2], tops_of[b - 2])
-        store_bottom(b - 2, bottom_of[b - 2])
-        hid_q[b, PHI] = quantise_hidden(waiting[2])
+        project(x_q[b], THETA, planes, (0, 1, 2, 3), HALF, True)
+        mirror(b - 2, *done[b - 2])
         grouped = hid.tile([P, PACK * S], BF16, align_bytes=256, name="grouped")
-        regroup(grouped[:], planes[:], WEIGHT_SPLIT)
-        hid_q[b, THETA] = quantise_hidden(grouped)
-        top_0 = score_top(b - 1, 0)
-        top_1 = score_top(b - 1, 1)
-        bottom = bottoms.tile([P, 2, S], F32, name="bottom")
-        score_bottom(b - 1, bottom)
-        top_2 = score_top(b, 0)
-        top_3 = score_top(b, 1)
-        mirror(bottom, [top_0, top_1])
-        store_bottom(b - 1, bottom)
-        bottom = bottoms.tile([P, 2, S], F32, name="bottom")
-        score_bottom(b, bottom)
-        mirror(bottom, [top_2, top_3])
-        store_bottom(b, bottom)
+        hid_q[b, THETA] = new_hidden()
+        halves = (slice(0, HALF), slice(HALF, S))
+        regroup(grouped[:, 0 : PACK * HALF], planes[:, :, halves[0]], THETA_SPLIT)
+        hid_q[b, PHI] = quantise_hidden(waiting[2])
+        regroup(grouped[:, PACK * HALF :], planes[:, :, halves[1]], THETA_SPLIT)
+        quantise_part(hid_q[b, THETA], grouped, halves[0])
+        quantise_part(hid_q[b, THETA], grouped, halves[1])
+        before = [score_row0(b - 1), score_rows13(b - 1), score_row2(b - 1)]
+        last = [score_row0(b), score_rows13(b)]
+        mirror(b - 1, *before)
+        last.append(score_row2(b))
+        mirror(b, *last)

@@ -45,19 +45,22 @@ def tile_selfattention_pa_t_kernel(tc, audio_feature, W_phi, b_phi, W_theta, b_t
         ends = ctx.enter_context(tc.tile_pool(name="ends", bufs=4))
         tops = ctx.enter_context(tc.tile_pool(name="tops", bufs=4))
         lows = ctx.enter_context(tc.tile_pool(name="lows", bufs=3))
-        warm = const.tile([P, 1], F32)
-        nc.vector.memset(warm[:], 0.0)
-        nc.scalar.activation(out=warm[:], in_=warm[:], func=ACT.Relu)
         psum_s = ctx.enter_context(tc.psum_pool(name="psum_s", bufs=4))
         psum_v = ctx.enter_context(tc.psum_pool(name="psum_v", bufs=4))
         ctx.enter_context(tc.manual_schedule())
 
-        bias_rows_bf = const.tile([P, P], BF16)
-        nc.vector.memset(bias_rows_bf[:], 0.0)
-        nc.scalar.dma_start(out=bias_rows_bf[0:H_TILES, :], in_=b_phi.rearrange("(m p) -> m p", p=P))
-        nc.scalar.dma_start(
-            out=bias_rows_bf[H_TILES : 2 * H_TILES, :], in_=b_theta.rearrange("(m p) -> m p", p=P)
-        )
+        warm = const.tile([P, 1], F32)
+        nc.vector.memset(warm[:], 0.0)
+        nc.scalar.activation(out=warm[:], in_=warm[:], func=ACT.Relu)
+        zeros = const.tile([P, S], BF16)
+        nc.vector.memset(zeros[:], 0.0)
+        idle = psum_v.tile([P, S], F32, tag="bank", name="idle")
+
+        def keep_tensor_busy(count):
+            for turn in range(count):
+                nc.tensor.matmul(idle[:], lhsT=zeros[:, 0:P], rhs=zeros[:], start=True, stop=True)
+
+        keep_tensor_busy(14)
 
         def load_weight(weight):
             w_raw = w_stage.tile([P, D_PASSES * PACK, H], BF16, name="w_raw")
@@ -76,6 +79,12 @@ def tile_selfattention_pa_t_kernel(tc, audio_feature, W_phi, b_phi, W_theta, b_t
             return x_sb
 
         w_raws = [load_weight(W_phi)]
+        bias_rows_bf = const.tile([P, P], BF16)
+        nc.vector.memset(bias_rows_bf[:], 0.0)
+        nc.sync.dma_start(out=bias_rows_bf[0:H_TILES, :], in_=b_phi.rearrange("(m p) -> m p", p=P))
+        nc.sync.dma_start(
+            out=bias_rows_bf[H_TILES : 2 * H_TILES, :], in_=b_theta.rearrange("(m p) -> m p", p=P)
+        )
         x_tiles = [load_x(0)]
         w_raws.append(load_weight(W_theta))
         for b in range(1, B):
@@ -141,6 +150,7 @@ def tile_selfattention_pa_t_kernel(tc, audio_feature, W_phi, b_phi, W_theta, b_t
                     else:
                         nc.vector.tensor_copy(out=dst, in_=src)
                 if then is not None:
+                    keep_tensor_busy(1)
                     then(x_grouped, half * HALF, HALF)
             return x_grouped
 
@@ -270,8 +280,8 @@ def tile_selfattention_pa_t_kernel(tc, audio_feature, W_phi, b_phi, W_theta, b_t
             nc.sync.dma_start(out=out[b, P : 2 * P, 0:P], in_=low21[:, HALF : 3 * P])
             nc.sync.dma_start(out=out[b, 3 * P : S, 0 : 3 * P], in_=low3[:])
 
-        spread_biases()
         quantise_weight(PHI)
+        spread_biases()
         x_q = {0: new_x_q()}
         transpose_x(0, lambda grouped, first, count: quantise_x(x_q[0], grouped, first, count))
         quantise_weight(THETA)

@@ -30,6 +30,8 @@ FLOPS = 2 * B * S * D * (2 * H) + 2 * B * S * S * H
 
 WEIGHT_SPLIT = 336
 THETA_SPLIT = 208
+VECTOR_FIRST = ((THETA, PHI), (PHI, THETA))
+SCALAR_FIRST = ((PHI, THETA), (THETA, PHI))
 SCORE_LAG = 3
 
 
@@ -60,7 +62,7 @@ def tile_selfattention_pa_t_kernel(tc, audio_feature, W_phi, b_phi, W_theta, b_t
             for turn in range(count):
                 nc.tensor.matmul(idle[:], lhsT=zeros[:, 0:P], rhs=zeros[:], start=True, stop=True)
 
-        keep_tensor_busy(14)
+        keep_tensor_busy(9)
 
         def load_weight(weight):
             w_raw = w_stage.tile([P, D_PASSES * PACK, H], BF16, name="w_raw")
@@ -232,20 +234,22 @@ def tile_selfattention_pa_t_kernel(tc, audio_feature, W_phi, b_phi, W_theta, b_t
                 out=dst, in0=bank_v, scalar=0.0, in1=relu_a[:], op0=ALU.max, op1=ALU.add
             )
 
-        def score_row0(b):
+        def score_row0(b, order=VECTOR_FIRST):
             bank_s = psum_s.tile([P, S], F32, tag="bank", name="prod_s")
             bank_v = psum_v.tile([P, S], F32, tag="bank", name="prod_v")
-            score_pass(bank_s[:], hid_q[b, PHI], 0, hid_q[b, THETA], 0, S)
-            score_pass(bank_v[:], hid_q[b, THETA], 0, hid_q[b, PHI], 0, S)
+            for stationary, moving in order:
+                bank = bank_s if stationary == PHI else bank_v
+                score_pass(bank[:], hid_q[b, stationary], 0, hid_q[b, moving], 0, S)
             r0 = tops.tile([P, S], F32, name="r0")
             relu_sum(r0[:], bank_s[:], bank_v[:])
             nc.sync.dma_start(out=out[b, 0:P, :], in_=r0[:])
             return r0
 
-        def score_rows13(b):
+        def score_rows13(b, order=VECTOR_FIRST):
             bank_s = psum_s.tile([P, S], F32, tag="bank", name="prod_s")
             bank_v = psum_v.tile([P, S], F32, tag="bank", name="prod_v")
-            for bank, stationary, moving in ((bank_s, PHI, THETA), (bank_v, THETA, PHI)):
+            for stationary, moving in order:
+                bank = bank_s if stationary == PHI else bank_v
                 score_pass(bank[:, 0:HALF], hid_q[b, stationary], 1, hid_q[b, moving], P, HALF)
                 score_pass(bank[:, HALF : 3 * P], hid_q[b, stationary], 1, hid_q[b, moving], 3 * P, P)
                 score_pass(bank[:, 3 * P : S], hid_q[b, stationary], 3, hid_q[b, moving], 3 * P, P)
@@ -255,11 +259,12 @@ def tile_selfattention_pa_t_kernel(tc, audio_feature, W_phi, b_phi, W_theta, b_t
             nc.sync.dma_start(out=out[b, 3 * P : S, 3 * P : S], in_=r13[:, 3 * P : S])
             return r13
 
-        def score_row2(b):
+        def score_row2(b, order=VECTOR_FIRST):
             bank_s = psum_s.tile([P, S], F32, tag="bank", name="prod_s")
             bank_v = psum_v.tile([P, S], F32, tag="bank", name="prod_v")
-            score_pass(bank_s[:, 0:HALF], hid_q[b, PHI], 2, hid_q[b, THETA], HALF, HALF)
-            score_pass(bank_v[:, 0:HALF], hid_q[b, THETA], 2, hid_q[b, PHI], HALF, HALF)
+            for stationary, moving in order:
+                bank = bank_s if stationary == PHI else bank_v
+                score_pass(bank[:, 0:HALF], hid_q[b, stationary], 2, hid_q[b, moving], HALF, HALF)
             r2 = tops.tile([P, HALF], F32, name="r2")
             relu_sum(r2[:], bank_s[:, 0:HALF], bank_v[:, 0:HALF])
             nc.sync.dma_start(out=out[b, HALF : HALF + P, HALF:S], in_=r2[:])
@@ -341,7 +346,7 @@ def tile_selfattention_pa_t_kernel(tc, audio_feature, W_phi, b_phi, W_theta, b_t
         quantise_part(hid_q[b, THETA], grouped, halves[0])
         quantise_part(hid_q[b, THETA], grouped, halves[1])
         before = [score_row0(b - 1), score_rows13(b - 1), score_row2(b - 1)]
-        last = [score_row0(b), score_rows13(b)]
+        last = [score_row0(b, SCALAR_FIRST), score_rows13(b, SCALAR_FIRST)]
         mirror(b - 1, *before)
-        last.append(score_row2(b))
+        last.append(score_row2(b, SCALAR_FIRST))
         mirror(b, *last)

@@ -30,6 +30,7 @@ FLOPS = 2 * B * S * D * (2 * H) + 2 * B * S * S * H
 
 WEIGHT_SPLIT = 336
 THETA_SPLIT = 208
+X_AHEAD = 4
 VECTOR_FIRST = ((THETA, PHI), (PHI, THETA))
 SCALAR_FIRST = ((PHI, THETA), (THETA, PHI))
 SCORE_LAG = 3
@@ -40,13 +41,14 @@ def tile_selfattention_pa_t_kernel(tc, audio_feature, W_phi, b_phi, W_theta, b_t
     with ExitStack() as ctx:
         const = ctx.enter_context(tc.tile_pool(name="const", bufs=1))
         w_stage = ctx.enter_context(tc.tile_pool(name="w_stage", bufs=2))
-        x_in = ctx.enter_context(tc.tile_pool(name="x_in", bufs=B))
+        x_in = ctx.enter_context(tc.tile_pool(name="x_in", bufs=X_AHEAD))
         x_mx = ctx.enter_context(tc.tile_pool(name="x_mx", bufs=2))
-        hid = ctx.enter_context(tc.tile_pool(name="hid", bufs=3))
+        hid = ctx.enter_context(tc.tile_pool(name="hid", bufs=4))
         hid_mx = ctx.enter_context(tc.tile_pool(name="hid_mx", bufs=6))
-        ends = ctx.enter_context(tc.tile_pool(name="ends", bufs=4))
-        tops = ctx.enter_context(tc.tile_pool(name="tops", bufs=4))
-        lows = ctx.enter_context(tc.tile_pool(name="lows", bufs=3))
+        ends = ctx.enter_context(tc.tile_pool(name="ends", bufs=8))
+        tops = ctx.enter_context(tc.tile_pool(name="tops", bufs=B))
+        full_rows = ctx.enter_context(tc.tile_pool(name="rows", bufs=ROW_TILES))
+        lows = ctx.enter_context(tc.tile_pool(name="lows", bufs=B))
         psum_s = ctx.enter_context(tc.psum_pool(name="psum_s", bufs=4))
         psum_v = ctx.enter_context(tc.psum_pool(name="psum_v", bufs=4))
         ctx.enter_context(tc.manual_schedule())
@@ -89,7 +91,7 @@ def tile_selfattention_pa_t_kernel(tc, audio_feature, W_phi, b_phi, W_theta, b_t
         )
         x_tiles = [load_x(0)]
         w_raws.append(load_weight(W_theta))
-        for b in range(1, B):
+        for b in range(1, X_AHEAD):
             x_tiles.append(load_x(b))
 
         ident = const.tile([P, P], F32)
@@ -270,6 +272,16 @@ def tile_selfattention_pa_t_kernel(tc, audio_feature, W_phi, b_phi, W_theta, b_t
             nc.sync.dma_start(out=out[b, HALF : HALF + P, HALF:S], in_=r2[:])
             return r2
 
+        def score_full_row(b, i, order):
+            bank_s = psum_s.tile([P, S], F32, tag="bank", name="prod_s")
+            bank_v = psum_v.tile([P, S], F32, tag="bank", name="prod_v")
+            for stationary, moving in order:
+                bank = bank_s if stationary == PHI else bank_v
+                score_pass(bank[:], hid_q[b, stationary], i, hid_q[b, moving], 0, S)
+            row = full_rows.tile([P, S], F32, name="row")
+            relu_sum(row[:], bank_s[:], bank_v[:])
+            nc.sync.dma_start(out=out[b, i * P : (i + 1) * P, :], in_=row[:])
+
         def mirror(b, r0, r13, r2):
             low21 = lows.tile([P, 3 * P], F32, name="low21")
             low3 = lows.tile([P, 3 * P], F32, name="low3")
@@ -289,6 +301,7 @@ def tile_selfattention_pa_t_kernel(tc, audio_feature, W_phi, b_phi, W_theta, b_t
         spread_biases()
         x_q = {0: new_x_q()}
         transpose_x(0, lambda grouped, first, count: quantise_x(x_q[0], grouped, first, count))
+        x_tiles.append(load_x(X_AHEAD))
         quantise_weight(THETA)
         hid_q = {}
         done = {}
@@ -305,6 +318,8 @@ def tile_selfattention_pa_t_kernel(tc, audio_feature, W_phi, b_phi, W_theta, b_t
                 project(x_q[b], w, planes, (1,))
             if w == PHI and b + 1 < B:
                 x_grouped = transpose_x(b + 1)
+                if b + 1 + X_AHEAD < B:
+                    x_tiles.append(load_x(b + 1 + X_AHEAD))
                 if scored > 0:
                     mirror(scored - 1, *done[scored - 1])
             if waiting is not None and w == PHI:
@@ -346,7 +361,8 @@ def tile_selfattention_pa_t_kernel(tc, audio_feature, W_phi, b_phi, W_theta, b_t
         quantise_part(hid_q[b, THETA], grouped, halves[0])
         quantise_part(hid_q[b, THETA], grouped, halves[1])
         before = [score_row0(b - 1), score_rows13(b - 1), score_row2(b - 1)]
-        last = [score_row0(b, SCALAR_FIRST), score_rows13(b, SCALAR_FIRST)]
+        score_full_row(b, 0, SCALAR_FIRST)
+        score_full_row(b, 1, SCALAR_FIRST)
+        score_full_row(b, 2, SCALAR_FIRST)
+        score_full_row(b, 3, SCALAR_FIRST)
         mirror(b - 1, *before)
-        last.append(score_row2(b, SCALAR_FIRST))
-        mirror(b, *last)

@@ -31,6 +31,7 @@ FLOPS = 2 * B * S * D * (2 * H) + 2 * B * S * S * H
 WEIGHT_SPLIT = 336
 THETA_SPLIT = 208
 X_AHEAD = 4
+RUN = 8
 VECTOR_FIRST = ((THETA, PHI), (PHI, THETA))
 SCALAR_FIRST = ((PHI, THETA), (THETA, PHI))
 SCORE_LAG = 3
@@ -115,8 +116,8 @@ def tile_selfattention_pa_t_kernel(tc, audio_feature, W_phi, b_phi, W_theta, b_t
         def regroup(dst, src, split):
             def view(first, last):
                 return dict(
-                    out=dst[:, PACK * first : PACK * last].rearrange("p (c i t) -> p c t i", i=4, t=PACK),
-                    in_=src[:, :, first:last].rearrange("p t (c i) -> p c t i", i=4),
+                    out=dst[:, PACK * first : PACK * last].rearrange("p (c i t) -> p c t i", i=RUN, t=PACK),
+                    in_=src[:, :, first:last].rearrange("p t (c i) -> p c t i", i=RUN),
                 )
 
             nc.vector.tensor_copy(**view(0, split))

@@ -43,8 +43,8 @@ def tile_selfattention_pa_t_kernel(tc, audio_feature, W_phi, b_phi, W_theta, b_t
         const = ctx.enter_context(tc.tile_pool(name="const", bufs=1))
         w_stage = ctx.enter_context(tc.tile_pool(name="w_stage", bufs=2))
         x_in = ctx.enter_context(tc.tile_pool(name="x_in", bufs=X_AHEAD))
-        x_mx = ctx.enter_context(tc.tile_pool(name="x_mx", bufs=2))
-        hid = ctx.enter_context(tc.tile_pool(name="hid", bufs=4))
+        x_mx = ctx.enter_context(tc.tile_pool(name="x_mx", bufs=3))
+        hid = ctx.enter_context(tc.tile_pool(name="hid", bufs=3))
         hid_mx = ctx.enter_context(tc.tile_pool(name="hid_mx", bufs=6))
         ends = ctx.enter_context(tc.tile_pool(name="ends", bufs=8))
         tops = ctx.enter_context(tc.tile_pool(name="tops", bufs=B))
@@ -305,30 +305,36 @@ def tile_selfattention_pa_t_kernel(tc, audio_feature, W_phi, b_phi, W_theta, b_t
         x_tiles.append(load_x(X_AHEAD))
         quantise_weight(THETA)
         hid_q = {}
+        to_quantise = []
         done = {}
         waiting = None
         for step in range(2 * B - 1):
             b, w = divmod(step, 2)
             scored, part = divmod(step - SCORE_LAG, 2)
-            x_grouped = None
+            turned = []
+            if w == PHI and b + 1 < B:
+                turned = [1] if b == 0 else [b + 1, b + 2] if b % 2 == 1 else []
             planes = hid.tile([P, H_TILES, S], BF16, name="planes")
             if step == 0:
                 project(x_q[b], w, planes, (0, 1, 2, 3), HALF)
             else:
                 project(x_q[b], w, planes, (0,))
                 project(x_q[b], w, planes, (1,))
-            if w == PHI and b + 1 < B:
-                x_grouped = transpose_x(b + 1)
-                if b + 1 + X_AHEAD < B:
-                    x_tiles.append(load_x(b + 1 + X_AHEAD))
-                if scored > 0:
-                    mirror(scored - 1, *done[scored - 1])
+            for t in turned:
+                to_quantise.append((t, transpose_x(t)))
+                if t + X_AHEAD < B:
+                    x_tiles.append(load_x(t + X_AHEAD))
+            if turned:
+                for c in sorted(done):
+                    if c < scored:
+                        mirror(c, *done.pop(c))
             if waiting is not None and w == PHI:
                 hid_q[waiting[0], waiting[1]] = quantise_hidden(waiting[2])
                 waiting = None
-            if x_grouped is not None:
-                x_q[b + 1] = new_x_q()
-                quantise_x(x_q[b + 1], x_grouped)
+            if w == PHI and to_quantise:
+                t, x_grouped = to_quantise.pop(0)
+                x_q[t] = new_x_q()
+                quantise_x(x_q[t], x_grouped)
             if step > 0:
                 project(x_q[b], w, planes, (2,))
             if scored >= 0:
@@ -336,8 +342,10 @@ def tile_selfattention_pa_t_kernel(tc, audio_feature, W_phi, b_phi, W_theta, b_t
                     done[scored] = [score_row0(scored)]
                 else:
                     done[scored].append(score_row2(scored))
-                    if x_grouped is None:
-                        mirror(scored - 1, *done[scored - 1])
+                    if b == B - 1:
+                        for c in sorted(done):
+                            if c < scored:
+                                mirror(c, *done.pop(c))
             if waiting is not None:
                 hid_q[waiting[0], waiting[1]] = quantise_hidden(waiting[2])
                 waiting = None

@@ -28,8 +28,8 @@ HALF_OVER_SQRT_D = 0.5 / math.sqrt(D)
 FLOPS = 2 * B * S * D * (2 * H) + 2 * B * S * S * H
 
 
-WEIGHT_SPLIT = 336
-THETA_SPLIT = 208
+WEIGHT_SPLIT = (336, 384)
+THETA_SPLIT = 256
 X_AHEAD = 4
 RUN = 8
 VECTOR_FIRST = ((THETA, PHI), (PHI, THETA))
@@ -48,8 +48,8 @@ def tile_selfattention_pa_t_kernel(tc, audio_feature, W_phi, b_phi, W_theta, b_t
         hid_mx = ctx.enter_context(tc.tile_pool(name="hid_mx", bufs=6))
         ends = ctx.enter_context(tc.tile_pool(name="ends", bufs=8))
         tops = ctx.enter_context(tc.tile_pool(name="tops", bufs=B))
-        full_rows = ctx.enter_context(tc.tile_pool(name="rows", bufs=ROW_TILES))
-        lows = ctx.enter_context(tc.tile_pool(name="lows", bufs=B))
+        full_rows = ctx.enter_context(tc.tile_pool(name="rows", bufs=ROW_TILES + 2))
+        lows = ctx.enter_context(tc.tile_pool(name="lows", bufs=4))
         psum_s = ctx.enter_context(tc.psum_pool(name="psum_s", bufs=4))
         psum_v = ctx.enter_context(tc.psum_pool(name="psum_v", bufs=4))
         ctx.enter_context(tc.manual_schedule())
@@ -124,11 +124,25 @@ def tile_selfattention_pa_t_kernel(tc, audio_feature, W_phi, b_phi, W_theta, b_t
             if split < src.shape[2]:
                 nc.scalar.copy(**view(split, src.shape[2]))
 
+        def regroup_shared(dst, src, split):
+            nc.vector.tensor_copy(
+                out=dst[:, 0 : PACK * split].rearrange("p (c i t) -> p c t i", i=RUN, t=PACK),
+                in_=src[:, :, 0:split].rearrange("p t (c i) -> p c t i", i=RUN),
+            )
+            n = src.shape[2]
+            if split < n:
+                first = split - 8
+                nc.gpsimd.tensor_scalar(
+                    out=dst[:, PACK * first :].rearrange("p (n t) -> p n t", t=PACK),
+                    in0=src[:, :, first:].rearrange("p t n -> p n t"),
+                    scalar1=1.0, scalar2=0.0, op0=ALU.mult, op1=ALU.add,
+                )
+
         def quantise_weight(w):
             w_grouped = []
             for g in range(D_PASSES):
                 w_grouped.append(w_stage.tile([P, PACK * H], BF16, align_bytes=256, name="w_grouped"))
-                regroup(w_grouped[g][:], w_raws[w][:, PACK * g : PACK * (g + 1), :], WEIGHT_SPLIT)
+                regroup(w_grouped[g][:], w_raws[w][:, PACK * g : PACK * (g + 1), :], WEIGHT_SPLIT[w])
             for g in range(D_PASSES):
                 nc.vector.quantize_mx(
                     out=w_codes[:, w, g, :].bitcast(FP8X4), scales=w_scales[:, w, g, :], in_=w_grouped[g][:]
@@ -273,31 +287,98 @@ def tile_selfattention_pa_t_kernel(tc, audio_feature, W_phi, b_phi, W_theta, b_t
             nc.sync.dma_start(out=out[b, HALF : HALF + P, HALF:S], in_=r2[:])
             return r2
 
-        def score_full_row(b, i, order):
-            bank_s = psum_s.tile([P, S], F32, tag="bank", name="prod_s")
-            bank_v = psum_v.tile([P, S], F32, tag="bank", name="prod_v")
-            for stationary, moving in order:
-                bank = bank_s if stationary == PHI else bank_v
-                score_pass(bank[:], hid_q[b, stationary], i, hid_q[b, moving], 0, S)
-            row = full_rows.tile([P, S], F32, name="row")
-            relu_sum(row[:], bank_s[:], bank_v[:])
-            nc.sync.dma_start(out=out[b, i * P : (i + 1) * P, :], in_=row[:])
+        def score_full_row(b, i, order, pieces=1):
+            width = S // pieces
+            for first in range(0, S, width):
+                cols = slice(first, first + width)
+                bank_s = psum_s.tile([P, S], F32, tag="bank", name="prod_s")
+                bank_v = psum_v.tile([P, S], F32, tag="bank", name="prod_v")
+                for stationary, moving in order:
+                    bank = bank_s if stationary == PHI else bank_v
+                    score_pass(bank[:, 0:width], hid_q[b, stationary], i, hid_q[b, moving], first, width)
+                row = full_rows.tile([P, S], F32, name="row")
+                relu_sum(row[:, 0:width], bank_s[:, 0:width], bank_v[:, 0:width])
+                nc.sync.dma_start(out=out[b, i * P : (i + 1) * P, cols], in_=row[:, 0:width])
 
         def mirror(b, r0, r13, r2):
             low21 = lows.tile([P, 3 * P], F32, name="low21")
             low3 = lows.tile([P, 3 * P], F32, name="low3")
-            for low, blocks in (
+            for piece, (low, blocks) in enumerate((
                 (low21, (r0[:, 2 * P : 3 * P], r13[:, P : 2 * P], r0[:, P : 2 * P])),
                 (low3, (r0[:, 3 * P : S], r13[:, 2 * P : 3 * P], r2[:, P : 2 * P])),
-            ):
-                bank = psum_s.tile([P, S], F32, tag="bank", name="turned")
+            )):
+                onv = False
+                bank = (psum_v if onv else psum_s).tile([P, S], F32, tag="bank", name="turned")
                 for i, block in enumerate(blocks):
                     nc.tensor.transpose(bank[:, i * P : (i + 1) * P], block, ident[:])
-                nc.scalar.copy(out=low[:], in_=bank[:, 0 : 3 * P])
+                if onv:
+                    nc.vector.tensor_copy(out=low[:], in_=bank[:, 0 : 3 * P])
+                else:
+                    nc.scalar.copy(out=low[:], in_=bank[:, 0 : 3 * P])
             nc.sync.dma_start(out=out[b, HALF : HALF + P, 0:HALF], in_=low21[:, 0:HALF])
             nc.sync.dma_start(out=out[b, P : 2 * P, 0:P], in_=low21[:, HALF : 3 * P])
             nc.sync.dma_start(out=out[b, 3 * P : S, 0 : 3 * P], in_=low3[:])
 
+
+        def project_T(x_q, w, m):
+            acc = psum_s.tile([P, S], F32, tag="bank", name="acc")
+            cols = slice(m * P, (m + 1) * P)
+            for g in range(D_PASSES):
+                nc.tensor.matmul_mx(out=acc[:], lhsT=w_codes[:, w, g, cols].bitcast(FP8X4), lhsT_scale=w_scales[:, w, g, cols],
+                    rhs=x_q[0][:, g, :].bitcast(FP8X4), rhs_scale=x_q[1][:, g, :], start=(g == 0), stop=(g == D_PASSES - 1))
+            return acc
+
+        def direct_T(x_q, i):
+            acc = psum_v.tile([P, H_TILES, P], F32, tag="bank", name="direct")
+            rows = slice(i * P, (i + 1) * P)
+            for m in range(H_TILES):
+                cols = slice(m * P, (m + 1) * P)
+                for g in range(D_PASSES):
+                    nc.tensor.matmul_mx(out=acc[:, m, :], lhsT=w_codes[:, THETA, g, cols].bitcast(FP8X4), lhsT_scale=w_scales[:, THETA, g, cols],
+                        rhs=x_q[0][:, g, rows].bitcast(FP8X4), rhs_scale=x_q[1][:, g, rows], start=(g == 0), stop=(g == D_PASSES - 1))
+            return acc
+
+        def direct_V(acc, i, grouped):
+            nc.vector.tensor_tensor(
+                out=grouped[:, i * PACK * P : (i + 1) * PACK * P].rearrange("p (n m) -> p n m", m=PACK),
+                in0=acc[:].rearrange("p m n -> p n m"),
+                in1=bias[:, H_TILES : 2 * H_TILES].unsqueeze(1).to_broadcast([P, P, PACK]),
+                op=ALU.add,
+            )
+
+        def project_S(acc, w, m, planes):
+            nc.scalar.activation(out=planes[:, m, :], in_=acc[:], func=ACT.Identity,
+                bias=bias[:, w * H_TILES + m : w * H_TILES + m + 1], scale=out_scale[w])
+
+        PIECES = {0: [(0, 0, S, 0)], 13: [(1, P, HALF, 0), (1, 3 * P, P, HALF), (3, 3 * P, P, 3 * P)], 2: [(2, HALF, HALF, 0)]}
+
+        def score_T(b, which, order=VECTOR_FIRST):
+            bank_s = psum_s.tile([P, S], F32, tag="bank", name="prod_s")
+            bank_v = psum_v.tile([P, S], F32, tag="bank", name="prod_v")
+            for stationary, moving in order:
+                bank = bank_s if stationary == PHI else bank_v
+                for i, first, count, at in PIECES[which]:
+                    score_pass(bank[:, at : at + count], hid_q[b, stationary], i, hid_q[b, moving], first, count)
+            return bank_s, bank_v
+
+        def score_E(b, which, banks):
+            n = HALF if which == 2 else S
+            r = tops.tile([P, n], F32, name={0: "r0", 13: "r13", 2: "r2"}[which])
+            relu_sum(r[:], banks[0][:, 0:n], banks[1][:, 0:n])
+            if which == 0:
+                nc.sync.dma_start(out=out[b, 0:P, :], in_=r[:])
+            elif which == 13:
+                nc.sync.dma_start(out=out[b, P : 2 * P, P:S], in_=r[:, 0 : 3 * P])
+                nc.sync.dma_start(out=out[b, 3 * P : S, 3 * P : S], in_=r[:, 3 * P : S])
+            else:
+                nc.sync.dma_start(out=out[b, HALF : HALF + P, HALF:S], in_=r[:])
+            return r
+
+        ORDER = {
+            "P": "p0 e0 p1 e1 MI QH QX p2 e2 S2 E2 p3 e3 RG".split(),
+            "PT": "p0 e0 p1 e1 TR MI QH QX p2 e2 S2 E2 p3 e3 RG".split(),
+            "T": "p0 e0 p1 e1 p2 e2 S0 E0 QH p3 e3 RG S13 E13".split(),
+        }
         quantise_weight(PHI)
         spread_biases()
         x_q = {0: new_x_q()}
@@ -308,70 +389,84 @@ def tile_selfattention_pa_t_kernel(tc, audio_feature, W_phi, b_phi, W_theta, b_t
         to_quantise = []
         done = {}
         waiting = None
+        fresh = None
+        banks = {}
+        accs = {}
+        pend = []
         for step in range(2 * B - 1):
             b, w = divmod(step, 2)
             scored, part = divmod(step - SCORE_LAG, 2)
-            turned = []
-            if w == PHI and b + 1 < B:
-                turned = [1] if b == 0 else [b + 1, b + 2] if b % 2 == 1 else []
-            planes = hid.tile([P, H_TILES, S], BF16, name="planes")
+            turned = [b + 1] if w == PHI else []
+            turned = [t for t in turned if t < B]
+            direct = w == THETA and False
+            if direct:
+                dgrouped = hid.tile([P, PACK * S], BF16, align_bytes=256, name="grouped")
+            else:
+                planes = hid.tile([P, H_TILES, S], BF16, name="planes")
+            kind = ('TD' if direct else 'T') if w == THETA else ('PT' if turned else 'P')
             if step == 0:
                 project(x_q[b], w, planes, (0, 1, 2, 3), HALF)
-            else:
-                project(x_q[b], w, planes, (0,))
-                project(x_q[b], w, planes, (1,))
-            for t in turned:
-                to_quantise.append((t, transpose_x(t)))
-                if t + X_AHEAD < B:
-                    x_tiles.append(load_x(t + X_AHEAD))
-            if turned:
-                for c in sorted(done):
-                    if c < scored:
-                        mirror(c, *done.pop(c))
-            if waiting is not None and w == PHI:
-                hid_q[waiting[0], waiting[1]] = quantise_hidden(waiting[2])
-                waiting = None
-            if w == PHI and to_quantise:
-                t, x_grouped = to_quantise.pop(0)
-                x_q[t] = new_x_q()
-                quantise_x(x_q[t], x_grouped)
-            if step > 0:
-                project(x_q[b], w, planes, (2,))
-            if scored >= 0:
-                if part == 0:
-                    done[scored] = [score_row0(scored)]
-                else:
-                    done[scored].append(score_row2(scored))
-                    if b == B - 1:
-                        for c in sorted(done):
-                            if c < scored:
-                                mirror(c, *done.pop(c))
-            if waiting is not None:
-                hid_q[waiting[0], waiting[1]] = quantise_hidden(waiting[2])
-                waiting = None
-            if step > 0:
-                project(x_q[b], w, planes, (3,))
-            grouped = hid.tile([P, PACK * S], BF16, align_bytes=256, name="grouped")
-            regroup(grouped[:], planes[:], S)
-            waiting = (b, w, grouped)
-            if scored >= 0 and part == 0:
-                done[scored].append(score_rows13(scored))
-
+            for it in ORDER[kind]:
+                if it[0] == 'p' and step > 0:
+                    accs[it[1]] = project_T(x_q[b], w, int(it[1]))
+                elif it[0] == 'e' and step > 0:
+                    project_S(accs[it[1]], w, int(it[1]), planes)
+                elif it[0] == 'd':
+                    accs[it] = direct_T(x_q[b], int(it[1]))
+                elif it[0] == 'x':
+                    direct_V(accs['d' + it[1]], int(it[1]), dgrouped)
+                elif it == 'RD':
+                    waiting = (b, w, dgrouped)
+                elif it == 'TR':
+                    for t in turned:
+                        to_quantise.append((t, transpose_x(t)))
+                        if t + X_AHEAD < B:
+                            x_tiles.append(load_x(t + X_AHEAD))
+                elif it == 'MI' and (turned or b == B - 1):
+                    for c in sorted(done):
+                        if c < scored and len(done[c]) == 3:
+                            mirror(c, *done.pop(c))
+                elif it == 'QH' and waiting is not None:
+                    hid_q[waiting[0], waiting[1]] = quantise_hidden(waiting[2])
+                    waiting = None
+                elif it == 'QX' and to_quantise:
+                    t, x_grouped = to_quantise.pop(0)
+                    x_q[t] = new_x_q()
+                    quantise_x(x_q[t], x_grouped)
+                elif it[0] == 'S' and scored >= 0:
+                    banks[it[1:]] = score_T(scored, int(it[1:]))
+                elif it[0] == 'E' and scored >= 0:
+                    done.setdefault(scored, []).append(score_E(scored, int(it[1:]), banks[it[1:]]))
+                elif it in ('RG', 'RL'):
+                    src = (b, w, planes) if it == 'RG' else fresh
+                    if src is not None:
+                        grouped = hid.tile([P, PACK * S], BF16, align_bytes=256, name="grouped")
+                        regroup_shared(grouped[:], src[2][:], (512, 512)[src[1]])
+                        waiting = (src[0], src[1], grouped)
+            fresh = (b, w, planes)
         b = B - 1
-        planes = hid.tile([P, H_TILES, S], BF16, name="planes")
-        project(x_q[b], THETA, planes, (0, 1, 2, 3), HALF, True)
-        mirror(b - 2, *done[b - 2])
-        grouped = hid.tile([P, PACK * S], BF16, align_bytes=256, name="grouped")
-        hid_q[b, THETA] = new_hidden()
-        halves = (slice(0, HALF), slice(HALF, S))
-        regroup(grouped[:, 0 : PACK * HALF], planes[:, :, halves[0]], THETA_SPLIT)
-        hid_q[b, PHI] = quantise_hidden(waiting[2])
-        regroup(grouped[:, PACK * HALF :], planes[:, :, halves[1]], THETA_SPLIT)
-        quantise_part(hid_q[b, THETA], grouped, halves[0])
-        quantise_part(hid_q[b, THETA], grouped, halves[1])
-        before = [score_row0(b - 1), score_rows13(b - 1), score_row2(b - 1)]
-        score_full_row(b, 0, SCALAR_FIRST)
-        score_full_row(b, 1, SCALAR_FIRST)
-        score_full_row(b, 2, SCALAR_FIRST)
-        score_full_row(b, 3, SCALAR_FIRST)
-        mirror(b - 1, *before)
+        if True:
+            planes = hid.tile([P, H_TILES, S], BF16, name="planes")
+            grouped = hid.tile([P, PACK * S], BF16, align_bytes=256, name="grouped")
+            hid_q[b, THETA] = new_hidden()
+            halves = (slice(0, HALF), slice(HALF, S))
+            before = []
+            for it in "PJ MI R0 QP R1 q0 q1 S0 S1 S2 F0 F1 F2 F3 MJ".split():
+                k, n = it[0], it[1:]
+                if it == 'PJ':
+                    project(x_q[b], THETA, planes, (0, 1, 2, 3), HALF, True)
+                elif it == 'MI':
+                    mirror(b - 2, *done.pop(b - 2))
+                elif k == 'R':
+                    i = int(n)
+                    regroup(grouped[:, PACK * HALF * i : PACK * HALF * (i + 1)], planes[:, :, halves[i]], THETA_SPLIT)
+                elif it == 'QP':
+                    hid_q[b, PHI] = quantise_hidden(waiting[2])
+                elif k == 'q':
+                    quantise_part(hid_q[b, THETA], grouped, halves[int(n)])
+                elif k == 'S':
+                    before.append((score_row0, score_rows13, score_row2)[int(n)](b - 1))
+                elif k == 'F':
+                    score_full_row(b, int(n), SCALAR_FIRST)
+                elif it == 'MJ':
+                    mirror(b - 1, *before)

@@ -78,9 +78,11 @@ def tile_selfattention_pa_t_kernel(tc, audio_feature, W_phi, b_phi, W_theta, b_t
 
         def load_x(b):
             x_sb = x_in.tile([P, ROW_TILES, D], BF16, name="x_sb")
-            rows = audio_feature[b].rearrange("(r p) d -> p r d", p=P)
+            rows = audio_feature[b].rearrange("(half p rr) d -> p half (rr d)", p=P, rr=2)
             for half in range(2):
-                nc.sync.dma_start(out=x_sb[:, 2 * half : 2 * half + 2, :], in_=rows[:, 2 * half : 2 * half + 2, :])
+                nc.sync.dma_start(
+                    out=x_sb[:, 2 * half : 2 * half + 2, :].rearrange("p rr d -> p (rr d)"), in_=rows[:, half, :]
+                )
             return x_sb
 
         w_raws = [load_weight(W_phi)]
@@ -162,8 +164,8 @@ def tile_selfattention_pa_t_kernel(tc, audio_feature, W_phi, b_phi, W_theta, b_t
                                 xt[:, u, rr * P : (rr + 1) * P], words[:, first : first + P], ident[:]
                             )
                     dst = x_grouped[:, g, half * 2 * K_PASS : (half + 1) * 2 * K_PASS]
-                    dst = dst.bitcast(F32).rearrange("p (s u) -> p s u", u=2)
-                    src = xt[:].rearrange("p u s -> p s u")
+                    dst = dst.bitcast(F32).rearrange("w (p rr u) -> w p rr u", rr=2, u=2)
+                    src = xt[:].rearrange("w u (rr p) -> w p rr u", rr=2)
                     if on_scalar:
                         nc.scalar.copy(out=dst, in_=src)
                     else:

@@ -34,6 +34,7 @@ X_AHEAD = 4
 RUN = 8
 VECTOR_FIRST = ((THETA, PHI), (PHI, THETA))
 SCALAR_FIRST = ((PHI, THETA), (THETA, PHI))
+VECTOR_TURNED = 5
 SCORE_LAG = 3
 
 
@@ -49,7 +50,7 @@ def tile_selfattention_pa_t_kernel(tc, audio_feature, W_phi, b_phi, W_theta, b_t
         ends = ctx.enter_context(tc.tile_pool(name="ends", bufs=8))
         tops = ctx.enter_context(tc.tile_pool(name="tops", bufs=B))
         full_rows = ctx.enter_context(tc.tile_pool(name="rows", bufs=ROW_TILES + 2))
-        lows = ctx.enter_context(tc.tile_pool(name="lows", bufs=4))
+        lows = ctx.enter_context(tc.tile_pool(name="lows", bufs=3))
         psum_s = ctx.enter_context(tc.psum_pool(name="psum_s", bufs=4))
         psum_v = ctx.enter_context(tc.psum_pool(name="psum_v", bufs=4))
         ctx.enter_context(tc.manual_schedule())
@@ -259,7 +260,7 @@ def tile_selfattention_pa_t_kernel(tc, audio_feature, W_phi, b_phi, W_theta, b_t
             for stationary, moving in order:
                 bank = bank_s if stationary == PHI else bank_v
                 score_pass(bank[:], hid_q[b, stationary], 0, hid_q[b, moving], 0, S)
-            r0 = tops.tile([P, S], F32, name="r0")
+            r0 = tops.tile([P, S], F32, align_bytes=256, name="r0")
             relu_sum(r0[:], bank_s[:], bank_v[:])
             nc.sync.dma_start(out=out[b, 0:P, :], in_=r0[:])
             return r0
@@ -272,7 +273,7 @@ def tile_selfattention_pa_t_kernel(tc, audio_feature, W_phi, b_phi, W_theta, b_t
                 score_pass(bank[:, 0:HALF], hid_q[b, stationary], 1, hid_q[b, moving], P, HALF)
                 score_pass(bank[:, HALF : 3 * P], hid_q[b, stationary], 1, hid_q[b, moving], 3 * P, P)
                 score_pass(bank[:, 3 * P : S], hid_q[b, stationary], 3, hid_q[b, moving], 3 * P, P)
-            r13 = tops.tile([P, S], F32, name="r13")
+            r13 = tops.tile([P, S], F32, align_bytes=256, name="r13")
             relu_sum(r13[:], bank_s[:], bank_v[:])
             nc.sync.dma_start(out=out[b, P : 2 * P, P:S], in_=r13[:, 0 : 3 * P])
             nc.sync.dma_start(out=out[b, 3 * P : S, 3 * P : S], in_=r13[:, 3 * P : S])
@@ -284,7 +285,7 @@ def tile_selfattention_pa_t_kernel(tc, audio_feature, W_phi, b_phi, W_theta, b_t
             for stationary, moving in order:
                 bank = bank_s if stationary == PHI else bank_v
                 score_pass(bank[:, 0:HALF], hid_q[b, stationary], 2, hid_q[b, moving], HALF, HALF)
-            r2 = tops.tile([P, HALF], F32, name="r2")
+            r2 = tops.tile([P, HALF], F32, align_bytes=256, name="r2")
             relu_sum(r2[:], bank_s[:, 0:HALF], bank_v[:, 0:HALF])
             nc.sync.dma_start(out=out[b, HALF : HALF + P, HALF:S], in_=r2[:])
             return r2
@@ -303,6 +304,23 @@ def tile_selfattention_pa_t_kernel(tc, audio_feature, W_phi, b_phi, W_theta, b_t
                 nc.sync.dma_start(out=out[b, i * P : (i + 1) * P, cols], in_=row[:, 0:width])
 
         def mirror(b, r0, r13, r2):
+            if b < VECTOR_TURNED:
+                low0 = lows.tile([P, 3 * P], F32, align_bytes=256, name="low0")
+                nc.vector.transpose(out=low0[:, 0:P], in_=r0[:, P : 2 * P])
+                nc.vector.transpose(out=low0[:, P : 3 * P], in_=r0[:, 2 * P : S])
+                for a in range(P // 32):
+                    nc.sync.dma_start(
+                        out=out[b, P:S, 32 * a : 32 * (a + 1)].rearrange("(g u) v -> u g v", u=32),
+                        in_=low0[32 * a : 32 * (a + 1), :].rearrange("u (g v) -> u g v", v=32),
+                    )
+                low23 = lows.tile([P, 3 * P], F32, name="low23")
+                bank = psum_s.tile([P, S], F32, tag="bank", name="turned")
+                for i, block in enumerate((r13[:, P : 2 * P], r13[:, 2 * P : 3 * P], r2[:, P : 2 * P])):
+                    nc.tensor.transpose(bank[:, i * P : (i + 1) * P], block, ident[:])
+                nc.scalar.copy(out=low23[:], in_=bank[:, 0 : 3 * P])
+                nc.sync.dma_start(out=out[b, HALF : HALF + P, P:HALF], in_=low23[:, 0:P])
+                nc.sync.dma_start(out=out[b, 3 * P : S, P : 3 * P], in_=low23[:, P : 3 * P])
+                return
             low21 = lows.tile([P, 3 * P], F32, name="low21")
             low3 = lows.tile([P, 3 * P], F32, name="low3")
             for piece, (low, blocks) in enumerate((
@@ -365,7 +383,7 @@ def tile_selfattention_pa_t_kernel(tc, audio_feature, W_phi, b_phi, W_theta, b_t
 
         def score_E(b, which, banks):
             n = HALF if which == 2 else S
-            r = tops.tile([P, n], F32, name={0: "r0", 13: "r13", 2: "r2"}[which])
+            r = tops.tile([P, n], F32, align_bytes=256, name={0: "r0", 13: "r13", 2: "r2"}[which])
             relu_sum(r[:], banks[0][:, 0:n], banks[1][:, 0:n])
             if which == 0:
                 nc.sync.dma_start(out=out[b, 0:P, :], in_=r[:])

@@ -34,7 +34,8 @@ X_AHEAD = 4
 RUN = 8
 VECTOR_FIRST = ((THETA, PHI), (PHI, THETA))
 SCALAR_FIRST = ((PHI, THETA), (THETA, PHI))
-VECTOR_TURNED = 5
+SPREAD_FROM = 4
+VECTOR_TURNED = 4
 SCORE_LAG = 3
 
 
@@ -77,8 +78,26 @@ def tile_selfattention_pa_t_kernel(tc, audio_feature, W_phi, b_phi, W_theta, b_t
                 )
             return w_raw
 
+        def split_x(x_sb):
+            flat = x_sb[:].rearrange("p r d -> p (r d)")
+            plain = flat[:, 0 : ROW_TILES * K_PASS].rearrange("p (r d) -> p r d", d=K_PASS)
+            return plain, flat[:, ROW_TILES * K_PASS :]
+
         def load_x(b):
-            x_sb = x_in.tile([P, ROW_TILES, D], BF16, name="x_sb")
+            x_sb = x_in.tile([P, ROW_TILES, D], BF16, align_bytes=256, name="x_sb")
+            if b >= SPREAD_FROM:
+                plain, spread = split_x(x_sb)
+                rows = audio_feature[b].rearrange("(half p rr) d -> p half rr d", p=P, rr=2)
+                for half in range(2):
+                    nc.sync.dma_start(out=plain[:, 2 * half : 2 * half + 2, :], in_=rows[:, half, :, 0:K_PASS])
+                for u in range(2):
+                    for a in range(P // 32):
+                        first = K_PASS + 256 * u + 64 * a
+                        nc.sync.dma_start(
+                            out=spread[32 * a + u : 32 * (a + 1) : 2, :].rearrange("s (k j) -> s k j", j=64),
+                            in_=audio_feature[b][:, first : first + 64].rearrange("(k s) j -> s k j", s=16),
+                        )
+                return x_sb
             rows = audio_feature[b].rearrange("(half p rr) d -> p half (rr d)", p=P, rr=2)
             for half in range(2):
                 nc.sync.dma_start(
@@ -153,6 +172,21 @@ def tile_selfattention_pa_t_kernel(tc, audio_feature, W_phi, b_phi, W_theta, b_t
 
         def transpose_x(b, then=None):
             x_grouped = x_mx.tile([P, D_PASSES, PACK * S], BF16, align_bytes=256, name="x_grouped")
+            if b >= SPREAD_FROM:
+                plain, spread = split_x(x_tiles[b])
+                for half in range(2):
+                    xt = psum_s.tile([P, 2, 2 * P], F32, tag="bank", name="xt")
+                    for u in range(2):
+                        for rr in range(2):
+                            words = plain[:, 2 * half + rr, :].bitcast(F32)
+                            nc.tensor.transpose(xt[:, u, rr * P : (rr + 1) * P], words[:, u * P : (u + 1) * P], ident[:])
+                    dst = x_grouped[:, 0, half * 2 * K_PASS : (half + 1) * 2 * K_PASS]
+                    nc.scalar.copy(
+                        out=dst.bitcast(F32).rearrange("w (p rr u) -> w p rr u", rr=2, u=2),
+                        in_=xt[:].rearrange("w u (rr p) -> w p rr u", rr=2),
+                    )
+                nc.vector.transpose(out=x_grouped[:, 1, :].bitcast(F32), in_=spread.bitcast(F32))
+                return x_grouped
             for half in range(2):
                 for g in range(D_PASSES):
                     on_scalar = g == 0

@@ -34,7 +34,7 @@ X_AHEAD = 4
 RUN = 8
 VECTOR_FIRST = ((THETA, PHI), (PHI, THETA))
 SCALAR_FIRST = ((PHI, THETA), (THETA, PHI))
-SPREAD_FROM = 4
+SPREAD_FROM = 3
 VECTOR_TURNED = 4
 SCORE_LAG = 3
 
@@ -189,7 +189,7 @@ def tile_selfattention_pa_t_kernel(tc, audio_feature, W_phi, b_phi, W_theta, b_t
                 return x_grouped
             for half in range(2):
                 for g in range(D_PASSES):
-                    on_scalar = g == 0
+                    on_scalar = g == 0 or (half == 1 and b == SPREAD_FROM - 1)
                     xt = (psum_s if on_scalar else psum_v).tile([P, 2, 2 * P], F32, tag="bank", name="xt")
                     for u in range(2):
                         for rr in range(2):

@@ -34,8 +34,6 @@ X_AHEAD = 4
 RUN = 8
 VECTOR_FIRST = ((THETA, PHI), (PHI, THETA))
 SCALAR_FIRST = ((PHI, THETA), (THETA, PHI))
-SPREAD_FROM = 3
-VECTOR_TURNED = 4
 SCORE_LAG = 3
 
 
@@ -85,7 +83,7 @@ def tile_selfattention_pa_t_kernel(tc, audio_feature, W_phi, b_phi, W_theta, b_t
 
         def load_x(b):
             x_sb = x_in.tile([P, ROW_TILES, D], BF16, align_bytes=256, name="x_sb")
-            if b >= SPREAD_FROM:
+            if b >= 3:
                 plain, spread = split_x(x_sb)
                 rows = audio_feature[b].rearrange("(half p rr) d -> p half rr d", p=P, rr=2)
                 for half in range(2):
@@ -98,11 +96,21 @@ def tile_selfattention_pa_t_kernel(tc, audio_feature, W_phi, b_phi, W_theta, b_t
                             in_=audio_feature[b][:, first : first + 64].rearrange("(k s) j -> s k j", s=16),
                         )
                 return x_sb
+            if False:
+                words = x_sb[:].rearrange("p r d -> p (r d)").bitcast(F32)
+                src = audio_feature[b].bitcast(F32)
+                for g in range(D_PASSES):
+                    for a in range(4):
+                        for u in range(2):
+                            first = 128 * (2 * g + u) + 32 * a
+                            nc.sync.dma_start(
+                                out=words[32 * a + u : 32 * a + 32 : 2, 1024 * g : 1024 * (g + 1)].rearrange("s (k j) -> s k j", j=32),
+                                in_=src[:, first : first + 32].rearrange("(k s) j -> s k j", s=16),
+                            )
+                return x_sb
             rows = audio_feature[b].rearrange("(half p rr) d -> p half (rr d)", p=P, rr=2)
             for half in range(2):
-                nc.sync.dma_start(
-                    out=x_sb[:, 2 * half : 2 * half + 2, :].rearrange("p rr d -> p (rr d)"), in_=rows[:, half, :]
-                )
+                nc.sync.dma_start(out=x_sb[:, 2 * half : 2 * half + 2, :].rearrange("p rr d -> p (rr d)"), in_=rows[:, half, :])
             return x_sb
 
         w_raws = [load_weight(W_phi)]
@@ -172,24 +180,29 @@ def tile_selfattention_pa_t_kernel(tc, audio_feature, W_phi, b_phi, W_theta, b_t
 
         def transpose_x(b, then=None):
             x_grouped = x_mx.tile([P, D_PASSES, PACK * S], BF16, align_bytes=256, name="x_grouped")
-            if b >= SPREAD_FROM:
+            if b >= 3:
                 plain, spread = split_x(x_tiles[b])
                 for half in range(2):
-                    xt = psum_s.tile([P, 2, 2 * P], F32, tag="bank", name="xt")
+                    onv = half == 1 and False
+                    xt = (psum_v if onv else psum_s).tile([P, 2, 2 * P], F32, tag="bank", name="xt")
                     for u in range(2):
                         for rr in range(2):
                             words = plain[:, 2 * half + rr, :].bitcast(F32)
                             nc.tensor.transpose(xt[:, u, rr * P : (rr + 1) * P], words[:, u * P : (u + 1) * P], ident[:])
                     dst = x_grouped[:, 0, half * 2 * K_PASS : (half + 1) * 2 * K_PASS]
-                    nc.scalar.copy(
-                        out=dst.bitcast(F32).rearrange("w (p rr u) -> w p rr u", rr=2, u=2),
-                        in_=xt[:].rearrange("w u (rr p) -> w p rr u", rr=2),
-                    )
+                    (nc.vector.tensor_copy if onv else nc.scalar.copy)(out=dst.bitcast(F32).rearrange("w (p rr u) -> w p rr u", rr=2, u=2), in_=xt[:].rearrange("w u (rr p) -> w p rr u", rr=2))
                 nc.vector.transpose(out=x_grouped[:, 1, :].bitcast(F32), in_=spread.bitcast(F32))
+                return x_grouped
+            if False:
+                for g in range(D_PASSES):
+                    nc.vector.transpose(
+                        out=x_grouped[:, g, :].bitcast(F32),
+                        in_=x_tiles[b][:].rearrange("p r d -> p (r d)").bitcast(F32)[:, 1024 * g : 1024 * (g + 1)],
+                    )
                 return x_grouped
             for half in range(2):
                 for g in range(D_PASSES):
-                    on_scalar = g == 0 or (half == 1 and b == SPREAD_FROM - 1)
+                    on_scalar = g == 0
                     xt = (psum_s if on_scalar else psum_v).tile([P, 2, 2 * P], F32, tag="bank", name="xt")
                     for u in range(2):
                         for rr in range(2):
@@ -338,19 +351,30 @@ def tile_selfattention_pa_t_kernel(tc, audio_feature, W_phi, b_phi, W_theta, b_t
                 nc.sync.dma_start(out=out[b, i * P : (i + 1) * P, cols], in_=row[:, 0:width])
 
         def mirror(b, r0, r13, r2):
-            if b < VECTOR_TURNED:
+            if b < 5:
+                def put(low, first, i):
+                    for a in range(P // 32):
+                        nc.sync.dma_start(
+                            out=out[b, first * P : S, i * P + 32 * a : i * P + 32 * (a + 1)].rearrange("(g u) v -> u g v", u=32),
+                            in_=low[32 * a : 32 * (a + 1), :].rearrange("u (g v) -> u g v", v=32),
+                        )
+
                 low0 = lows.tile([P, 3 * P], F32, align_bytes=256, name="low0")
                 nc.vector.transpose(out=low0[:, 0:P], in_=r0[:, P : 2 * P])
                 nc.vector.transpose(out=low0[:, P : 3 * P], in_=r0[:, 2 * P : S])
-                for a in range(P // 32):
-                    nc.sync.dma_start(
-                        out=out[b, P:S, 32 * a : 32 * (a + 1)].rearrange("(g u) v -> u g v", u=32),
-                        in_=low0[32 * a : 32 * (a + 1), :].rearrange("u (g v) -> u g v", v=32),
-                    )
-                low23 = lows.tile([P, 3 * P], F32, name="low23")
+                put(low0, 1, 0)
+                if False:
+                    low1 = lows.tile([P, 2 * P], F32, align_bytes=256, name="low1")
+                    nc.vector.transpose(out=low1[:], in_=r13[:, P : 3 * P])
+                    put(low1, 2, 1)
+                    low2 = lows.tile([P, P], F32, align_bytes=256, name="low2")
+                    nc.vector.transpose(out=low2[:], in_=r2[:, P : 2 * P])
+                    put(low2, 3, 2)
+                    return
                 bank = psum_s.tile([P, S], F32, tag="bank", name="turned")
                 for i, block in enumerate((r13[:, P : 2 * P], r13[:, 2 * P : 3 * P], r2[:, P : 2 * P])):
                     nc.tensor.transpose(bank[:, i * P : (i + 1) * P], block, ident[:])
+                low23 = lows.tile([P, 3 * P], F32, name="low23")
                 nc.scalar.copy(out=low23[:], in_=bank[:, 0 : 3 * P])
                 nc.sync.dma_start(out=out[b, HALF : HALF + P, P:HALF], in_=low23[:, 0:P])
                 nc.sync.dma_start(out=out[b, 3 * P : S, P : 3 * P], in_=low23[:, P : 3 * P])
@@ -381,6 +405,25 @@ def tile_selfattention_pa_t_kernel(tc, audio_feature, W_phi, b_phi, W_theta, b_t
                 nc.tensor.matmul_mx(out=acc[:], lhsT=w_codes[:, w, g, cols].bitcast(FP8X4), lhsT_scale=w_scales[:, w, g, cols],
                     rhs=x_q[0][:, g, :].bitcast(FP8X4), rhs_scale=x_q[1][:, g, :], start=(g == 0), stop=(g == D_PASSES - 1))
             return acc
+
+        half_accs = []
+
+        def half_T(x_q, i):
+            for m in range(H_TILES):
+                if i == 0:
+                    acc = psum_s.tile([P, S], F32, tag="bank", name="acc")
+                    half_accs.append(acc)
+                cols = slice(m * P, (m + 1) * P)
+                rows = slice(i * HALF, (i + 1) * HALF)
+                for g in range(D_PASSES):
+                    nc.tensor.matmul_mx(out=half_accs[m][:, rows], lhsT=w_codes[:, THETA, g, cols].bitcast(FP8X4), lhsT_scale=w_scales[:, THETA, g, cols],
+                        rhs=x_q[0][:, g, rows].bitcast(FP8X4), rhs_scale=x_q[1][:, g, rows], start=(g == 0), stop=(g == D_PASSES - 1))
+
+        def half_E(planes, i):
+            rows = slice(i * HALF, (i + 1) * HALF)
+            for m in range(H_TILES):
+                nc.scalar.activation(out=planes[:, m, rows], in_=half_accs[m][:, rows], func=ACT.Identity,
+                    bias=bias[:, THETA * H_TILES + m : THETA * H_TILES + m + 1], scale=out_scale[THETA])
 
         def direct_T(x_q, i):
             acc = psum_v.tile([P, H_TILES, P], F32, tag="bank", name="direct")
@@ -429,9 +472,9 @@ def tile_selfattention_pa_t_kernel(tc, audio_feature, W_phi, b_phi, W_theta, b_t
             return r
 
         ORDER = {
-            "P": "p0 e0 p1 e1 MI QH QX p2 e2 S2 E2 p3 e3 RG".split(),
-            "PT": "p0 e0 p1 e1 TR MI QH QX p2 e2 S2 E2 p3 e3 RG".split(),
-            "T": "p0 e0 p1 e1 p2 e2 S0 E0 QH p3 e3 RG S13 E13".split(),
+            "P": "QH RL p0 e0 p1 e1 MI S2 E2 p2 e2 p3 e3".split(),
+            "PT": "QH RL p0 e0 p1 e1 TR S2 MI E2 p2 e2 p3 e3".split(),
+            "T": "QH QX RL p0 e0 p1 e1 p2 S0 e2 S13 E0 E13 p3 e3".split(),
         }
         quantise_weight(PHI)
         spread_biases()
@@ -458,6 +501,8 @@ def tile_selfattention_pa_t_kernel(tc, audio_feature, W_phi, b_phi, W_theta, b_t
             else:
                 planes = hid.tile([P, H_TILES, S], BF16, name="planes")
             kind = ('TD' if direct else 'T') if w == THETA else ('PT' if turned else 'P')
+            if b == B - 1 and 'L' in ORDER:
+                kind = 'L'
             if step == 0:
                 project(x_q[b], w, planes, (0, 1, 2, 3), HALF)
             for it in ORDER[kind]:
@@ -476,6 +521,8 @@ def tile_selfattention_pa_t_kernel(tc, audio_feature, W_phi, b_phi, W_theta, b_t
                         to_quantise.append((t, transpose_x(t)))
                         if t + X_AHEAD < B:
                             x_tiles.append(load_x(t + X_AHEAD))
+                elif it == 'ML':
+                    mirror(scored, *done.pop(scored))
                 elif it == 'MI' and (turned or b == B - 1):
                     for c in sorted(done):
                         if c < scored and len(done[c]) == 3:
@@ -495,7 +542,10 @@ def tile_selfattention_pa_t_kernel(tc, audio_feature, W_phi, b_phi, W_theta, b_t
                     src = (b, w, planes) if it == 'RG' else fresh
                     if src is not None:
                         grouped = hid.tile([P, PACK * S], BF16, align_bytes=256, name="grouped")
-                        regroup_shared(grouped[:], src[2][:], (512, 512)[src[1]])
+                        if 416 < S:
+                            regroup_shared(grouped[:], src[2][:], 416)
+                        else:
+                            regroup(grouped[:], src[2][:], S)
                         waiting = (src[0], src[1], grouped)
             fresh = (b, w, planes)
         b = B - 1
@@ -504,16 +554,27 @@ def tile_selfattention_pa_t_kernel(tc, audio_feature, W_phi, b_phi, W_theta, b_t
             grouped = hid.tile([P, PACK * S], BF16, align_bytes=256, name="grouped")
             hid_q[b, THETA] = new_hidden()
             halves = (slice(0, HALF), slice(HALF, S))
-            before = []
-            for it in "PJ MI R0 QP R1 q0 q1 S0 S1 S2 F0 F1 F2 F3 MJ".split():
+            before = done.pop(b - 1, [])
+            for it in "P0 X0 QL P1 X1 GL MI R0 QP R1 q0 q1 S0 S1 S2 F0 F1 F2 F3 MJ".split():
                 k, n = it[0], it[1:]
                 if it == 'PJ':
                     project(x_q[b], THETA, planes, (0, 1, 2, 3), HALF, True)
+                elif k == 'P':
+                    half_T(x_q[b], int(n))
+                elif k == 'X':
+                    half_E(planes, int(n))
                 elif it == 'MI':
-                    mirror(b - 2, *done.pop(b - 2))
+                    if b - 2 in done:
+                        mirror(b - 2, *done.pop(b - 2))
                 elif k == 'R':
                     i = int(n)
                     regroup(grouped[:, PACK * HALF * i : PACK * HALF * (i + 1)], planes[:, :, halves[i]], THETA_SPLIT)
+                elif it == 'QL':
+                    hid_q[waiting[0], waiting[1]] = quantise_hidden(waiting[2])
+                elif it == 'GL':
+                    tail_phi = hid.tile([P, PACK * S], BF16, align_bytes=256, name="grouped")
+                    regroup_shared(tail_phi[:], fresh[2][:], S)
+                    waiting = (b, PHI, tail_phi)
                 elif it == 'QP':
                     hid_q[b, PHI] = quantise_hidden(waiting[2])
                 elif k == 'q':

import math
from contextlib import ExitStack

import concourse.mybir as mybir
from concourse.masks import make_identity

F32 = mybir.dt.float32
BF16 = mybir.dt.bfloat16
U32 = mybir.dt.uint32
U8 = mybir.dt.uint8
FP8X4 = mybir.dt.float8_e4m3fn_x4
ACT = mybir.ActivationFunctionType
ALU = mybir.AluOpType

P = 128
PACK = 4
K_PASS = P * PACK

B, S, D, H = 8, 512, 1024, 512
D_PASSES = D // K_PASS
ROW_TILES = S // P
HALF = S // 2
H_TILES = H // P
assert H_TILES == PACK
PHI, THETA = 0, 1
HALF_OVER_SQRT_D = 0.5 / math.sqrt(D)

FLOPS = 2 * B * S * D * (2 * H) + 2 * B * S * S * H


WEIGHT_SPLIT = (336, 384)
THETA_SPLIT = 256
X_AHEAD = 4
RUN = 8
VECTOR_FIRST = ((THETA, PHI), (PHI, THETA))
SCALAR_FIRST = ((PHI, THETA), (THETA, PHI))
SCORE_LAG = 3


def tile_selfattention_pa_t_kernel(tc, audio_feature, W_phi, b_phi, W_theta, b_theta, out):
    nc = tc.nc
    with ExitStack() as ctx:
        const = ctx.enter_context(tc.tile_pool(name="const", bufs=1))
        w_stage = ctx.enter_context(tc.tile_pool(name="w_stage", bufs=2))
        x_in = ctx.enter_context(tc.tile_pool(name="x_in", bufs=X_AHEAD))
        x_mx = ctx.enter_context(tc.tile_pool(name="x_mx", bufs=3))
        hid = ctx.enter_context(tc.tile_pool(name="hid", bufs=3))
        hid_mx = ctx.enter_context(tc.tile_pool(name="hid_mx", bufs=6))
        ends = ctx.enter_context(tc.tile_pool(name="ends", bufs=8))
        tops = ctx.enter_context(tc.tile_pool(name="tops", bufs=B))
        full_rows = ctx.enter_context(tc.tile_pool(name="rows", bufs=ROW_TILES + 2))
        lows = ctx.enter_context(tc.tile_pool(name="lows", bufs=3))
        psum_s = ctx.enter_context(tc.psum_pool(name="psum_s", bufs=4))
        psum_v = ctx.enter_context(tc.psum_pool(name="psum_v", bufs=4))
        ctx.enter_context(tc.manual_schedule())

        warm = const.tile([P, 1], F32)
        nc.vector.memset(warm[:], 0.0)
        nc.scalar.activation(out=warm[:], in_=warm[:], func=ACT.Relu)
        zeros = const.tile([P, S], BF16)
        nc.vector.memset(zeros[:], 0.0)
        idle = psum_v.tile([P, S], F32, tag="bank", name="idle")

        def keep_tensor_busy(count):
            for turn in range(count):
                nc.tensor.matmul(idle[:], lhsT=zeros[:, 0:P], rhs=zeros[:], start=True, stop=True)

        keep_tensor_busy(9)

        def load_weight(weight):
            w_raw = w_stage.tile([P, D_PASSES * PACK, H], BF16, name="w_raw")
            for g in range(D_PASSES):
                nc.sync.dma_start(
                    out=w_raw[:, PACK * g : PACK * (g + 1), :].rearrange("q (u e) h -> q u (e h)", e=2),
                    in_=weight[K_PASS * g : K_PASS * (g + 1), :].rearrange("(u q e) h -> q u (e h)", q=P, e=2),
                )
            return w_raw

        def split_x(x_sb):
            flat = x_sb[:].rearrange("p r d -> p (r d)")
            plain = flat[:, 0 : ROW_TILES * K_PASS].rearrange("p (r d) -> p r d", d=K_PASS)
            return plain, flat[:, ROW_TILES * K_PASS :]

        def load_x(b):
            x_sb = x_in.tile([P, ROW_TILES, D], BF16, align_bytes=256, name="x_sb")
            if b >= 3:
                plain, spread = split_x(x_sb)
                rows = audio_feature[b].rearrange("(half p rr) d -> p half rr d", p=P, rr=2)
                for half in range(2):
                    nc.sync.dma_start(out=plain[:, 2 * half : 2 * half + 2, :], in_=rows[:, half, :, 0:K_PASS])
                for u in range(2):
                    for a in range(P // 32):
                        first = K_PASS + 256 * u + 64 * a
                        nc.sync.dma_start(
                            out=spread[32 * a + u : 32 * (a + 1) : 2, :].rearrange("s (k j) -> s k j", j=64),
                            in_=audio_feature[b][:, first : first + 64].rearrange("(k s) j -> s k j", s=16),
                        )
                return x_sb
            if False:
                words = x_sb[:].rearrange("p r d -> p (r d)").bitcast(F32)
                src = audio_feature[b].bitcast(F32)
                for g in range(D_PASSES):
                    for a in range(4):
                        for u in range(2):
                            first = 128 * (2 * g + u) + 32 * a
                            nc.sync.dma_start(
                                out=words[32 * a + u : 32 * a + 32 : 2, 1024 * g : 1024 * (g + 1)].rearrange("s (k j) -> s k j", j=32),
                                in_=src[:, first : first + 32].rearrange("(k s) j -> s k j", s=16),
                            )
                return x_sb
            rows = audio_feature[b].rearrange("(half p rr) d -> p half (rr d)", p=P, rr=2)
            for half in range(2):
                nc.sync.dma_start(out=x_sb[:, 2 * half : 2 * half + 2, :].rearrange("p rr d -> p (rr d)"), in_=rows[:, half, :])
            return x_sb

        w_raws = [load_weight(W_phi)]
        bias_rows_bf = const.tile([P, P], BF16)
        nc.vector.memset(bias_rows_bf[:], 0.0)
        nc.sync.dma_start(out=bias_rows_bf[0:H_TILES, :], in_=b_phi.rearrange("(m p) -> m p", p=P))
        nc.sync.dma_start(
            out=bias_rows_bf[H_TILES : 2 * H_TILES, :], in_=b_theta.rearrange("(m p) -> m p", p=P)
        )
        x_tiles = [load_x(0)]
        w_raws.append(load_weight(W_theta))
        for b in range(1, X_AHEAD):
            x_tiles.append(load_x(b))

        ident = const.tile([P, P], F32)
        make_identity(nc, ident[:])

        bias = const.tile([P, 2 * H_TILES], F32)

        def spread_biases():
            bias_rows = const.tile([P, P], F32)
            nc.scalar.copy(out=bias_rows[:], in_=bias_rows_bf[:])
            bias_t = psum_s.tile([P, P], F32, tag="bank")
            nc.tensor.transpose(bias_t[:], bias_rows[:], ident[:])
            nc.scalar.mul(out=bias[:, 0:H_TILES], in_=bias_t[:, 0:H_TILES], mul=HALF_OVER_SQRT_D)
            nc.scalar.copy(out=bias[:, H_TILES : 2 * H_TILES], in_=bias_t[:, H_TILES : 2 * H_TILES])

        out_scale = [HALF_OVER_SQRT_D, 1.0]

        w_codes = const.tile([P, 2, D_PASSES, H], U32, align_bytes=256)
        w_scales = const.tile([P, 2, D_PASSES, H], U8, align_bytes=256)

        def regroup(dst, src, split):
            def view(first, last):
                return dict(
                    out=dst[:, PACK * first : PACK * last].rearrange("p (c i t) -> p c t i", i=RUN, t=PACK),
                    in_=src[:, :, first:last].rearrange("p t (c i) -> p c t i", i=RUN),
                )

            nc.vector.tensor_copy(**view(0, split))
            if split < src.shape[2]:
                nc.scalar.copy(**view(split, src.shape[2]))

        def regroup_shared(dst, src, split):
            nc.vector.tensor_copy(
                out=dst[:, 0 : PACK * split].rearrange("p (c i t) -> p c t i", i=RUN, t=PACK),
                in_=src[:, :, 0:split].rearrange("p t (c i) -> p c t i", i=RUN),
            )
            n = src.shape[2]
            if split < n:
                first = split - 8
                nc.gpsimd.tensor_scalar(
                    out=dst[:, PACK * first :].rearrange("p (n t) -> p n t", t=PACK),
                    in0=src[:, :, first:].rearrange("p t n -> p n t"),
                    scalar1=1.0, scalar2=0.0, op0=ALU.mult, op1=ALU.add,
                )

        def quantise_weight(w):
            w_grouped = []
            for g in range(D_PASSES):
                w_grouped.append(w_stage.tile([P, PACK * H], BF16, align_bytes=256, name="w_grouped"))
                regroup(w_grouped[g][:], w_raws[w][:, PACK * g : PACK * (g + 1), :], WEIGHT_SPLIT[w])
            for g in range(D_PASSES):
                nc.vector.quantize_mx(
                    out=w_codes[:, w, g, :].bitcast(FP8X4), scales=w_scales[:, w, g, :], in_=w_grouped[g][:]
                )

        def transpose_x(b, then=None):
            x_grouped = x_mx.tile([P, D_PASSES, PACK * S], BF16, align_bytes=256, name="x_grouped")
            if b >= 3:
                plain, spread = split_x(x_tiles[b])
                for half in range(2):
                    onv = half == 1 and False
                    xt = (psum_v if onv else psum_s).tile([P, 2, 2 * P], F32, tag="bank", name="xt")
                    for u in range(2):
                        for rr in range(2):
                            words = plain[:, 2 * half + rr, :].bitcast(F32)
                            nc.tensor.transpose(xt[:, u, rr * P : (rr + 1) * P], words[:, u * P : (u + 1) * P], ident[:])
                    dst = x_grouped[:, 0, half * 2 * K_PASS : (half + 1) * 2 * K_PASS]
                    (nc.vector.tensor_copy if onv else nc.scalar.copy)(out=dst.bitcast(F32).rearrange("w (p rr u) -> w p rr u", rr=2, u=2), in_=xt[:].rearrange("w u (rr p) -> w p rr u", rr=2))
                nc.vector.transpose(out=x_grouped[:, 1, :].bitcast(F32), in_=spread.bitcast(F32))
                return x_grouped
            if False:
                for g in range(D_PASSES):
                    nc.vector.transpose(
                        out=x_grouped[:, g, :].bitcast(F32),
                        in_=x_tiles[b][:].rearrange("p r d -> p (r d)").bitcast(F32)[:, 1024 * g : 1024 * (g + 1)],
                    )
                return x_grouped
            for half in range(2):
                for g in range(D_PASSES):
                    on_scalar = g == 0
                    xt = (psum_s if on_scalar else psum_v).tile([P, 2, 2 * P], F32, tag="bank", name="xt")
                    for u in range(2):
                        for rr in range(2):
                            words = x_tiles[b][:, 2 * half + rr, :].bitcast(F32)
                            first = (2 * g + u) * P
                            nc.tensor.transpose(
                                xt[:, u, rr * P : (rr + 1) * P], words[:, first : first + P], ident[:]
                            )
                    dst = x_grouped[:, g, half * 2 * K_PASS : (half + 1) * 2 * K_PASS]
                    dst = dst.bitcast(F32).rearrange("w (p rr u) -> w p rr u", rr=2, u=2)
                    src = xt[:].rearrange("w u (rr p) -> w p rr u", rr=2)
                    if on_scalar:
                        nc.scalar.copy(out=dst, in_=src)
                    else:
                        nc.vector.tensor_copy(out=dst, in_=src)
                if then is not None:
                    keep_tensor_busy(1)
                    then(x_grouped, half * HALF, HALF)
            return x_grouped

        def new_x_q():
            x_codes = x_mx.tile([P, D_PASSES, S], U32, align_bytes=256, name="x_codes")
            x_scales = x_mx.tile([P, D_PASSES, S], U8, align_bytes=256, name="x_scales")
            return x_codes, x_scales

        def quantise_x(x_q, x_grouped, first=0, count=S):
            for g in range(D_PASSES):
                nc.vector.quantize_mx(
                    out=x_q[0][:, g, first : first + count].bitcast(FP8X4),
                    scales=x_q[1][:, g, first : first + count],
                    in_=x_grouped[:, g, PACK * first : PACK * (first + count)],
                )

        def project(x_q, w, planes, tiles, step=S, split_out=False):
            x_codes, x_scales = x_q
            accs = [psum_s.tile([P, S], F32, tag="bank", name="acc") for tile_m in tiles]
            for first in range(0, S, step):
                positions = slice(first, first + step)
                for acc, m in zip(accs, tiles):
                    cols = slice(m * P, (m + 1) * P)
                    for g in range(D_PASSES):
                        nc.tensor.matmul_mx(
                            out=acc[:, positions],
                            lhsT=w_codes[:, w, g, cols].bitcast(FP8X4),
                            lhsT_scale=w_scales[:, w, g, cols],
                            rhs=x_codes[:, g, positions].bitcast(FP8X4),
                            rhs_scale=x_scales[:, g, positions],
                            start=(g == 0),
                            stop=(g == D_PASSES - 1),
                        )
                if split_out or first + step == S:
                    done_positions = positions if split_out else slice(0, S)
                    for acc, m in zip(accs, tiles):
                        nc.scalar.activation(
                            out=planes[:, m, done_positions],
                            in_=acc[:, done_positions],
                            func=ACT.Identity,
                            bias=bias[:, w * H_TILES + m : w * H_TILES + m + 1],
                            scale=out_scale[w],
                        )

        def new_hidden():
            codes = hid_mx.tile([P, S], U32, align_bytes=256, name="hid_codes")
            scales = hid_mx.tile([P, S], U8, align_bytes=256, name="hid_scales")
            return codes, scales

        def quantise_part(hidden, grouped, positions):
            nc.vector.quantize_mx(
                out=hidden[0][:, positions].bitcast(FP8X4),
                scales=hidden[1][:, positions],
                in_=grouped[:, PACK * positions.start : PACK * positions.stop],
            )

        def quantise_hidden(grouped):
            hidden = new_hidden()
            quantise_part(hidden, grouped, slice(0, S))
            return hidden

        def score_pass(dst, stationary, i, moving, first, count):
            rows = slice(i * P, (i + 1) * P)
            cols = slice(first, first + count)
            nc.tensor.matmul_mx(
                out=dst,
                lhsT=stationary[0][:, rows].bitcast(FP8X4),
                lhsT_scale=stationary[1][:, rows],
                rhs=moving[0][:, cols].bitcast(FP8X4),
                rhs_scale=moving[1][:, cols],
                start=True,
                stop=True,
            )

        def relu_sum(dst, bank_s, bank_v):
            relu_a = ends.tile(list(bank_s.shape), F32, tag="relu_a", name="relu_a")
            nc.scalar.activation(out=relu_a[:], in_=bank_s, func=ACT.Relu)
            nc.vector.scalar_tensor_tensor(
                out=dst, in0=bank_v, scalar=0.0, in1=relu_a[:], op0=ALU.max, op1=ALU.add
            )

        def score_row0(b, order=VECTOR_FIRST):
            bank_s = psum_s.tile([P, S], F32, tag="bank", name="prod_s")
            bank_v = psum_v.tile([P, S], F32, tag="bank", name="prod_v")
            for stationary, moving in order:
                bank = bank_s if stationary == PHI else bank_v
                score_pass(bank[:], hid_q[b, stationary], 0, hid_q[b, moving], 0, S)
            r0 = tops.tile([P, S], F32, align_bytes=256, name="r0")
            relu_sum(r0[:], bank_s[:], bank_v[:])
            nc.sync.dma_start(out=out[b, 0:P, :], in_=r0[:])
            return r0

        def score_rows13(b, order=VECTOR_FIRST):
            bank_s = psum_s.tile([P, S], F32, tag="bank", name="prod_s")
            bank_v = psum_v.tile([P, S], F32, tag="bank", name="prod_v")
            for stationary, moving in order:
                bank = bank_s if stationary == PHI else bank_v
                score_pass(bank[:, 0:HALF], hid_q[b, stationary], 1, hid_q[b, moving], P, HALF)
                score_pass(bank[:, HALF : 3 * P], hid_q[b, stationary], 1, hid_q[b, moving], 3 * P, P)
                score_pass(bank[:, 3 * P : S], hid_q[b, stationary], 3, hid_q[b, moving], 3 * P, P)
            r13 = tops.tile([P, S], F32, align_bytes=256, name="r13")
            relu_sum(r13[:], bank_s[:], bank_v[:])
            nc.sync.dma_start(out=out[b, P : 2 * P, P:S], in_=r13[:, 0 : 3 * P])
            nc.sync.dma_start(out=out[b, 3 * P : S, 3 * P : S], in_=r13[:, 3 * P : S])
            return r13

        def score_row2(b, order=VECTOR_FIRST):
            bank_s = psum_s.tile([P, S], F32, tag="bank", name="prod_s")
            bank_v = psum_v.tile([P, S], F32, tag="bank", name="prod_v")
            for stationary, moving in order:
                bank = bank_s if stationary == PHI else bank_v
                score_pass(bank[:, 0:HALF], hid_q[b, stationary], 2, hid_q[b, moving], HALF, HALF)
            r2 = tops.tile([P, HALF], F32, align_bytes=256, name="r2")
            relu_sum(r2[:], bank_s[:, 0:HALF], bank_v[:, 0:HALF])
            nc.sync.dma_start(out=out[b, HALF : HALF + P, HALF:S], in_=r2[:])
            return r2

        def score_full_row(b, i, order, pieces=1):
            width = S // pieces
            for first in range(0, S, width):
                cols = slice(first, first + width)
                bank_s = psum_s.tile([P, S], F32, tag="bank", name="prod_s")
                bank_v = psum_v.tile([P, S], F32, tag="bank", name="prod_v")
                for stationary, moving in order:
                    bank = bank_s if stationary == PHI else bank_v
                    score_pass(bank[:, 0:width], hid_q[b, stationary], i, hid_q[b, moving], first, width)
                row = full_rows.tile([P, S], F32, name="row")
                relu_sum(row[:, 0:width], bank_s[:, 0:width], bank_v[:, 0:width])
                nc.sync.dma_start(out=out[b, i * P : (i + 1) * P, cols], in_=row[:, 0:width])

        def mirror(b, r0, r13, r2):
            if b < 5:
                def put(low, first, i):
                    for a in range(P // 32):
                        nc.sync.dma_start(
                            out=out[b, first * P : S, i * P + 32 * a : i * P + 32 * (a + 1)].rearrange("(g u) v -> u g v", u=32),
                            in_=low[32 * a : 32 * (a + 1), :].rearrange("u (g v) -> u g v", v=32),
                        )

                low0 = lows.tile([P, 3 * P], F32, align_bytes=256, name="low0")
                nc.vector.transpose(out=low0[:, 0:P], in_=r0[:, P : 2 * P])
                nc.vector.transpose(out=low0[:, P : 3 * P], in_=r0[:, 2 * P : S])
                put(low0, 1, 0)
                if False:
                    low1 = lows.tile([P, 2 * P], F32, align_bytes=256, name="low1")
                    nc.vector.transpose(out=low1[:], in_=r13[:, P : 3 * P])
                    put(low1, 2, 1)
                    low2 = lows.tile([P, P], F32, align_bytes=256, name="low2")
                    nc.vector.transpose(out=low2[:], in_=r2[:, P : 2 * P])
                    put(low2, 3, 2)
                    return
                bank = psum_s.tile([P, S], F32, tag="bank", name="turned")
                for i, block in enumerate((r13[:, P : 2 * P], r13[:, 2 * P : 3 * P], r2[:, P : 2 * P])):
                    nc.tensor.transpose(bank[:, i * P : (i + 1) * P], block, ident[:])
                low23 = lows.tile([P, 3 * P], F32, name="low23")
                nc.scalar.copy(out=low23[:], in_=bank[:, 0 : 3 * P])
                nc.sync.dma_start(out=out[b, HALF : HALF + P, P:HALF], in_=low23[:, 0:P])
                nc.sync.dma_start(out=out[b, 3 * P : S, P : 3 * P], in_=low23[:, P : 3 * P])
                return
            low21 = lows.tile([P, 3 * P], F32, name="low21")
            low3 = lows.tile([P, 3 * P], F32, name="low3")
            for piece, (low, blocks) in enumerate((
                (low21, (r0[:, 2 * P : 3 * P], r13[:, P : 2 * P], r0[:, P : 2 * P])),
                (low3, (r0[:, 3 * P : S], r13[:, 2 * P : 3 * P], r2[:, P : 2 * P])),
            )):
                onv = False
                bank = (psum_v if onv else psum_s).tile([P, S], F32, tag="bank", name="turned")
                for i, block in enumerate(blocks):
                    nc.tensor.transpose(bank[:, i * P : (i + 1) * P], block, ident[:])
                if onv:
                    nc.vector.tensor_copy(out=low[:], in_=bank[:, 0 : 3 * P])
                else:
                    nc.scalar.copy(out=low[:], in_=bank[:, 0 : 3 * P])
            nc.sync.dma_start(out=out[b, HALF : HALF + P, 0:HALF], in_=low21[:, 0:HALF])
            nc.sync.dma_start(out=out[b, P : 2 * P, 0:P], in_=low21[:, HALF : 3 * P])
            nc.sync.dma_start(out=out[b, 3 * P : S, 0 : 3 * P], in_=low3[:])


        def project_T(x_q, w, m):
            acc = psum_s.tile([P, S], F32, tag="bank", name="acc")
            cols = slice(m * P, (m + 1) * P)
            for g in range(D_PASSES):
                nc.tensor.matmul_mx(out=acc[:], lhsT=w_codes[:, w, g, cols].bitcast(FP8X4), lhsT_scale=w_scales[:, w, g, cols],
                    rhs=x_q[0][:, g, :].bitcast(FP8X4), rhs_scale=x_q[1][:, g, :], start=(g == 0), stop=(g == D_PASSES - 1))
            return acc

        half_accs = []

        def half_T(x_q, i):
            for m in range(H_TILES):
                if i == 0:
                    acc = psum_s.tile([P, S], F32, tag="bank", name="acc")
                    half_accs.append(acc)
                cols = slice(m * P, (m + 1) * P)
                rows = slice(i * HALF, (i + 1) * HALF)
                for g in range(D_PASSES):
                    nc.tensor.matmul_mx(out=half_accs[m][:, rows], lhsT=w_codes[:, THETA, g, cols].bitcast(FP8X4), lhsT_scale=w_scales[:, THETA, g, cols],
                        rhs=x_q[0][:, g, rows].bitcast(FP8X4), rhs_scale=x_q[1][:, g, rows], start=(g == 0), stop=(g == D_PASSES - 1))

        def half_E(planes, i):
            rows = slice(i * HALF, (i + 1) * HALF)
            for m in range(H_TILES):
                nc.scalar.activation(out=planes[:, m, rows], in_=half_accs[m][:, rows], func=ACT.Identity,
                    bias=bias[:, THETA * H_TILES + m : THETA * H_TILES + m + 1], scale=out_scale[THETA])

        def direct_T(x_q, i):
            acc = psum_v.tile([P, H_TILES, P], F32, tag="bank", name="direct")
            rows = slice(i * P, (i + 1) * P)
            for m in range(H_TILES):
                cols = slice(m * P, (m + 1) * P)
                for g in range(D_PASSES):
                    nc.tensor.matmul_mx(out=acc[:, m, :], lhsT=w_codes[:, THETA, g, cols].bitcast(FP8X4), lhsT_scale=w_scales[:, THETA, g, cols],
                        rhs=x_q[0][:, g, rows].bitcast(FP8X4), rhs_scale=x_q[1][:, g, rows], start=(g == 0), stop=(g == D_PASSES - 1))
            return acc

        def direct_V(acc, i, grouped):
            nc.vector.tensor_tensor(
                out=grouped[:, i * PACK * P : (i + 1) * PACK * P].rearrange("p (n m) -> p n m", m=PACK),
                in0=acc[:].rearrange("p m n -> p n m"),
                in1=bias[:, H_TILES : 2 * H_TILES].unsqueeze(1).to_broadcast([P, P, PACK]),
                op=ALU.add,
            )

        def project_S(acc, w, m, planes):
            nc.scalar.activation(out=planes[:, m, :], in_=acc[:], func=ACT.Identity,
                bias=bias[:, w * H_TILES + m : w * H_TILES + m + 1], scale=out_scale[w])

        PIECES = {0: [(0, 0, S, 0)], 13: [(1, P, HALF, 0), (1, 3 * P, P, HALF), (3, 3 * P, P, 3 * P)], 2: [(2, HALF, HALF, 0)]}

        def score_T(b, which, order=VECTOR_FIRST):
            bank_s = psum_s.tile([P, S], F32, tag="bank", name="prod_s")
            bank_v = psum_v.tile([P, S], F32, tag="bank", name="prod_v")
            for stationary, moving in order:
                bank = bank_s if stationary == PHI else bank_v
                for i, first, count, at in PIECES[which]:
                    score_pass(bank[:, at : at + count], hid_q[b, stationary], i, hid_q[b, moving], first, count)
            return bank_s, bank_v

        def score_E(b, which, banks):
            n = HALF if which == 2 else S
            r = tops.tile([P, n], F32, align_bytes=256, name={0: "r0", 13: "r13", 2: "r2"}[which])
            relu_sum(r[:], banks[0][:, 0:n], banks[1][:, 0:n])
            if which == 0:
                nc.sync.dma_start(out=out[b, 0:P, :], in_=r[:])
            elif which == 13:
                nc.sync.dma_start(out=out[b, P : 2 * P, P:S], in_=r[:, 0 : 3 * P])
                nc.sync.dma_start(out=out[b, 3 * P : S, 3 * P : S], in_=r[:, 3 * P : S])
            else:
                nc.sync.dma_start(out=out[b, HALF : HALF + P, HALF:S], in_=r[:])
            return r

        ORDER = {
            "P": "QH RL p0 e0 p1 e1 MI S2 E2 p2 e2 p3 e3".split(),
            "PT": "QH RL p0 e0 p1 e1 TR S2 MI E2 p2 e2 p3 e3".split(),
            "T": "QH QX RL p0 e0 p1 e1 p2 S0 e2 S13 E0 E13 p3 e3".split(),
        }
        quantise_weight(PHI)
        spread_biases()
        x_q = {0: new_x_q()}
        transpose_x(0, lambda grouped, first, count: quantise_x(x_q[0], grouped, first, count))
        x_tiles.append(load_x(X_AHEAD))
        quantise_weight(THETA)
        hid_q = {}
        to_quantise = []
        done = {}
        waiting = None
        fresh = None
        banks = {}
        accs = {}
        pend = []
        for step in range(2 * B - 1):
            b, w = divmod(step, 2)
            scored, part = divmod(step - SCORE_LAG, 2)
            turned = [b + 1] if w == PHI else []
            turned = [t for t in turned if t < B]
            direct = w == THETA and False
            if direct:
                dgrouped = hid.tile([P, PACK * S], BF16, align_bytes=256, name="grouped")
            else:
                planes = hid.tile([P, H_TILES, S], BF16, name="planes")
            kind = ('TD' if direct else 'T') if w == THETA else ('PT' if turned else 'P')
            if b == B - 1 and 'L' in ORDER:
                kind = 'L'
            if step == 0:
                project(x_q[b], w, planes, (0, 1, 2, 3), HALF)
            for it in ORDER[kind]:
                if it[0] == 'p' and step > 0:
                    accs[it[1]] = project_T(x_q[b], w, int(it[1]))
                elif it[0] == 'e' and step > 0:
                    project_S(accs[it[1]], w, int(it[1]), planes)
                elif it[0] == 'd':
                    accs[it] = direct_T(x_q[b], int(it[1]))
                elif it[0] == 'x':
                    direct_V(accs['d' + it[1]], int(it[1]), dgrouped)
                elif it == 'RD':
                    waiting = (b, w, dgrouped)
                elif it == 'TR':
                    for t in turned:
                        to_quantise.append((t, transpose_x(t)))
                        if t + X_AHEAD < B:
                            x_tiles.append(load_x(t + X_AHEAD))
                elif it == 'ML':
                    mirror(scored, *done.pop(scored))
                elif it == 'MI' and (turned or b == B - 1):
                    for c in sorted(done):
                        if c < scored and len(done[c]) == 3:
                            mirror(c, *done.pop(c))
                elif it == 'QH' and waiting is not None:
                    hid_q[waiting[0], waiting[1]] = quantise_hidden(waiting[2])
                    waiting = None
                elif it == 'QX' and to_quantise:
                    t, x_grouped = to_quantise.pop(0)
                    x_q[t] = new_x_q()
                    quantise_x(x_q[t], x_grouped)
                elif it[0] == 'S' and scored >= 0:
                    banks[it[1:]] = score_T(scored, int(it[1:]))
                elif it[0] == 'E' and scored >= 0:
                    done.setdefault(scored, []).append(score_E(scored, int(it[1:]), banks[it[1:]]))
                elif it in ('RG', 'RL'):
                    src = (b, w, planes) if it == 'RG' else fresh
                    if src is not None:
                        grouped = hid.tile([P, PACK * S], BF16, align_bytes=256, name="grouped")
                        if 416 < S:
                            regroup_shared(grouped[:], src[2][:], 416)
                        else:
                            regroup(grouped[:], src[2][:], S)
                        waiting = (src[0], src[1], grouped)
            fresh = (b, w, planes)
        b = B - 1
        if True:
            planes = hid.tile([P, H_TILES, S], BF16, name="planes")
            grouped = hid.tile([P, PACK * S], BF16, align_bytes=256, name="grouped")
            hid_q[b, THETA] = new_hidden()
            halves = (slice(0, HALF), slice(HALF, S))
            before = done.pop(b - 1, [])
            for it in "P0 X0 QL P1 X1 GL MI R0 QP R1 q0 q1 S0 S1 S2 F0 F1 F2 F3 MJ".split():
                k, n = it[0], it[1:]
                if it == 'PJ':
                    project(x_q[b], THETA, planes, (0, 1, 2, 3), HALF, True)
                elif k == 'P':
                    half_T(x_q[b], int(n))
                elif k == 'X':
                    half_E(planes, int(n))
                elif it == 'MI':
                    if b - 2 in done:
                        mirror(b - 2, *done.pop(b - 2))
                elif k == 'R':
                    i = int(n)
                    regroup(grouped[:, PACK * HALF * i : PACK * HALF * (i + 1)], planes[:, :, halves[i]], THETA_SPLIT)
                elif it == 'QL':
                    hid_q[waiting[0], waiting[1]] = quantise_hidden(waiting[2])
                elif it == 'GL':
                    tail_phi = hid.tile([P, PACK * S], BF16, align_bytes=256, name="grouped")
                    regroup_shared(tail_phi[:], fresh[2][:], S)
                    waiting = (b, PHI, tail_phi)
                elif it == 'QP':
                    hid_q[b, PHI] = quantise_hidden(waiting[2])
                elif k == 'q':
                    quantise_part(hid_q[b, THETA], grouped, halves[int(n)])
                elif k == 'S':
                    before.append((score_row0, score_rows13, score_row2)[int(n)](b - 1))
                elif k == 'F':
                    score_full_row(b, int(n), SCALAR_FIRST)
                elif it == 'MJ':
                    mirror(b - 1, *before)
